import numpy as np
import ml_dtypes


def mxq(x, axis, fmt="e4m3"):
    dtype, down = {"e4m3": (ml_dtypes.float8_e4m3fn, 7), "e5m2": (ml_dtypes.float8_e5m2, 14)}[fmt]
    v = np.moveaxis(np.asarray(x, np.float32).astype(ml_dtypes.bfloat16).astype(np.float64), axis, -1)
    blocks = v.reshape(v.shape[:-1] + (-1, 32))
    amax = np.abs(blocks).max(-1, keepdims=True)
    byte = np.maximum(np.where(amax > 0, np.frexp(amax)[1] - 1 + 127, 0) - down, 1)
    scale = np.exp2(byte - 127.0)
    codes = (blocks / scale).astype(np.float32).astype(dtype).astype(np.float64)
    return np.moveaxis((codes * scale).reshape(v.shape), -1, axis)


WIDE = False


def mx_kscale(k):
    if not WIDE:
        return np.ones(k)
    levels = np.array([10, -10, 5, -5, 0])
    a = np.random.permutation(np.resize(levels, k // 512 * 4)).reshape(k // 512, 4)
    idx = np.arange(k)
    return np.exp2(a[idx // 512, idx % 128 // 32])


BF16 = ml_dtypes.bfloat16


def bf(x):
    return np.asarray(x, np.float32).astype(BF16)


def f64(x):
    return np.asarray(x).astype(np.float64)


N, MUL0, MUL1, MUL2, DIM1, DIM2 = 1024, 512, 256, 128, 3, 5
D_S = MUL0
D_V = MUL1 * DIM1
D_T = MUL2 * DIM2
N_GATES = MUL1 + MUL2


def sigmoid(v):
    return 1.0 / (1.0 + np.exp(-v))


def leaky_relu(v):
    return np.where(v >= 0.0, v, 0.01 * v)


def setup_inputs():
    k = mx_kscale(MUL0)
    x = np.random.standard_normal((N, D_S + D_V + D_T))
    x[:, :D_S] = x[:, :D_S] * k
    return {"x": bf(x), "W0": bf(np.random.standard_normal((MUL0, MUL0 + N_GATES)) / k[:, None]),
            "W1": bf(np.random.standard_normal((MUL1, MUL1))), "W2": bf(np.random.standard_normal((MUL2, MUL2)))}


def reference(x, W0, W1, W2):
    x = f64(x)
    n = x.shape[0]
    s = x[:, :D_S]
    v = x[:, D_S:D_S + D_V].reshape(n, MUL1, DIM1)
    t = x[:, D_S + D_V:].reshape(n, MUL2, DIM2)
    s_out = (mxq(s, 1, "e4m3") @ mxq(f64(W0), 0, "e4m3")) / np.sqrt(MUL0)
    v_out = (v.transpose(0, 2, 1) @ f64(W1)).transpose(0, 2, 1) / np.sqrt(MUL1)
    t_out = (t.transpose(0, 2, 1) @ f64(W2)).transpose(0, 2, 1) / np.sqrt(MUL2)
    scalars = leaky_relu(s_out[:, :MUL0])
    gates = sigmoid(s_out[:, MUL0:])
    gv = v_out * gates[:, :MUL1, None]
    gt = t_out * gates[:, MUL1:, None]
    return np.concatenate([scalars, gv.reshape(n, -1), gt.reshape(n, -1)], axis=-1)

@@ -1,0 +1,247 @@
+import math
+from contextlib import ExitStack
+
+import concourse.bass as bass
+import concourse.mybir as mybir
+import concourse.tile as tile
+from concourse.masks import make_identity
+
+BF16 = mybir.dt.bfloat16
+F32 = mybir.dt.float32
+U32 = mybir.dt.uint32
+U8 = mybir.dt.uint8
+FP8X4 = mybir.dt.float8_e4m3fn_x4
+ACT = mybir.ActivationFunctionType
+ALU = mybir.AluOpType
+
+P = 128
+NT = 8
+D = 1920
+FLOPS = 2 * 1024 * (512 * 896 + 3 * 256 * 256 + 5 * 128 * 128)
+
+PIN = True
+STRIDED = (0, 1)
+
+C0 = 1.0 / math.sqrt(512.0)
+C1 = 1.0 / 16.0
+C2 = 1.0 / math.sqrt(128.0)
+
+
+def tile_equivariantmlpblock_kernel(tc, x, W0, W1, W2, out):
+    nc = tc.nc
+    xv = x.rearrange("(p t) c -> p t c", t=NT)
+    ov = out.rearrange("(p t) c -> p t c", t=NT)
+    with ExitStack() as ctx:
+        keep = ctx.enter_context(tc.tile_pool(name="keep", bufs=1))
+        work = ctx.enter_context(tc.tile_pool(name="work", bufs=NT))
+        psum = ctx.enter_context(tc.psum_pool(name="psum", bufs=1))
+        if PIN:
+            ctx.enter_context(tc.manual_schedule())
+
+        xs = []
+        for j in range(NT):
+            xj = keep.tile([P, D], BF16, name="x%d" % j, align_bytes=64)
+            xs.append(xj)
+        w0raw = keep.tile([P, 4, 896], BF16, name="w0raw", align_bytes=64)
+        w1 = keep.tile([P, 2, 256], BF16, name="w1")
+        w2 = keep.tile([P, 128], BF16, name="w2")
+        nc.sync.dma_start(out=xs[0][:], in_=xv[:, 0, :])
+        nc.sync.dma_start(
+            out=w0raw[:].rearrange("p (u e) c -> p u (e c)", u=2),
+            in_=W0.rearrange("(u p e) c -> p u (e c)", u=2, p=P, e=2),
+        )
+        nc.sync.dma_start(out=w1[:], in_=W1.rearrange("(c i) o -> i c o", c=2))
+        nc.sync.dma_start(out=w2[:], in_=W2)
+        for j in range(1, NT):
+            nc.sync.dma_start(out=xs[j][:], in_=xv[:, j, :])
+
+        idf = keep.tile([P, P], F32, name="idf")
+        idb = keep.tile([P, P], BF16, name="idb")
+        make_identity(nc, idf[:])
+        make_identity(nc, idb[:])
+        warm = keep.tile([P, 1], F32, name="warm")
+        warm2 = keep.tile([P, 1], F32, name="warm2")
+        nc.vector.memset(warm[:], 0.0)
+        nc.scalar.activation(out=warm2[:], in_=warm[:], func=ACT.Sigmoid)
+
+        w0g = keep.tile([P, 896, 4], BF16, name="w0g", align_bytes=64)
+        w0c = keep.tile([P, 896], U32, name="w0c", align_bytes=64)
+        w0s = keep.tile([P, 896], U8, name="w0s", align_bytes=64)
+
+        def regroup(eng_copy, lo, hi):
+            eng_copy(
+                out=w0g[:, lo:hi, :].rearrange("p (c i) t -> p c t i", i=4),
+                in_=w0raw[:, :, lo:hi].rearrange("p t (c i) -> p c t i", i=4),
+            )
+
+        def quant_w(lo, hi):
+            nc.vector.quantize_mx(
+                out=w0c[:, lo:hi].bitcast(FP8X4),
+                scales=w0s[:, lo:hi],
+                in_=w0g[:, lo:hi, :].rearrange("p c t -> p (c t)"),
+            )
+
+        vd = {}
+        td = {}
+
+        def deint(j):
+            tdj = work.tile([P, 5, 128], BF16, name="td")
+            vdj = work.tile([P, 3, 256], BF16, name="vd")
+            nc.gpsimd.tensor_scalar(
+                out=tdj[:], in0=xs[j][:, 1280:1920].rearrange("p (i m) -> p m i", m=5),
+                scalar1=1.0, scalar2=0.0, op0=ALU.mult, op1=ALU.add)
+            nc.gpsimd.tensor_scalar(
+                out=vdj[:], in0=xs[j][:, 512:1280].rearrange("p (i m) -> p m i", m=3),
+                scalar1=1.0, scalar2=0.0, op0=ALU.mult, op1=ALU.add)
+            td[j] = tdj
+            vd[j] = vdj
+
+        def t_src(j, m):
+            if j in STRIDED:
+                return xs[j][:, 1280:1920].rearrange("p (i m) -> p m i", m=5)[:, m, :]
+            return td[j][:, m, :]
+
+        def v_src(j, m, c):
+            if j in STRIDED:
+                return xs[j][:, 512:1280].rearrange("p (i m) -> p m i", m=3)[:, m, 128 * c:128 * c + 128]
+            return vd[j][:, m, 128 * c:128 * c + 128]
+
+        ua = {}
+        ub = {}
+        sc = {}
+        ss = {}
+        gates = {}
+        osb = {}
+
+        def stage_T(j):
+            t1 = psum.tile([P, 1024], BF16, name="t1")
+            t2 = psum.tile([P, 1024], BF16, name="t2")
+            t1f = t1[:, 0:512].bitcast(F32)
+            xw = xs[j][:, 0:512].bitcast(F32)
+            for u in range(2):
+                nc.tensor.transpose(t1f[:, 128 * u:128 * u + 128], xw[:, 128 * u:128 * u + 128], idf[:])
+            for m in range(4):
+                nc.tensor.transpose(t1[:, 512 + 128 * m:640 + 128 * m], t_src(j, m), idb[:])
+            nc.tensor.transpose(t2[:, 0:128], t_src(j, 4), idb[:])
+            for m in range(3):
+                for c in range(2):
+                    q = 1 + 2 * m + c
+                    nc.tensor.transpose(t2[:, 128 * q:128 * q + 128], v_src(j, m, c), idb[:])
+            gs = work.tile([P, 512], BF16, name="gs", align_bytes=64)
+            nc.scalar.copy(
+                out=gs[:].bitcast(F32).rearrange("p (n u) -> p n u", u=2),
+                in_=t1f.rearrange("p (u n) -> p n u", u=2),
+            )
+            uaj = work.tile([P, 4, 128], BF16, name="ua")
+            ubj = work.tile([P, 7, 128], BF16, name="ub")
+            nc.scalar.copy(out=uaj[:].rearrange("p a n -> p (a n)"), in_=t1[:, 512:1024])
+            nc.scalar.copy(out=ubj[:].rearrange("p a n -> p (a n)"), in_=t2[:, 0:896])
+            scj = work.tile([P, 128], U32, name="sc", align_bytes=64)
+            ssj = work.tile([P, 128], U8, name="ss", align_bytes=64)
+            nc.vector.quantize_mx(out=scj[:].bitcast(FP8X4), scales=ssj[:], in_=gs[:])
+            ua[j] = uaj
+            ub[j] = ubj
+            sc[j] = scj
+            ss[j] = ssj
+
+        def mx(j, acc, lo, hi):
+            nc.tensor.matmul_mx(
+                out=acc, lhsT=sc[j][:].bitcast(FP8X4), lhsT_scale=ss[j][:],
+                rhs=w0c[:, lo:hi].bitcast(FP8X4), rhs_scale=w0s[:, lo:hi],
+                start=True, stop=True)
+
+        def stage_M(j):
+            pb = psum.tile([P, 512], F32, name="pb")
+            pa = psum.tile([P, 512], F32, name="pa")
+            mx(j, pb[:, 0:256], 512, 768)
+            mx(j, pb[:, 256:384], 768, 896)
+            mx(j, pa[:], 0, 512)
+            g = work.tile([P, 384], F32, name="g")
+            o = work.tile([P, D], F32, name="o")
+            nc.scalar.activation(out=g[:], in_=pb[:, 0:384], func=ACT.Sigmoid, scale=C0)
+            nc.scalar.activation(out=o[:, 0:512], in_=pa[:], func=ACT.Relu, scale=0.99 * C0)
+            gates[j] = g
+            osb[j] = o
+            return pa
+
+        def combine(j, pa):
+            o = osb[j]
+            nc.vector.scalar_tensor_tensor(
+                out=o[:, 0:512], in0=pa[:], scalar=0.01 * C0, in1=o[:, 0:512],
+                op0=ALU.mult, op1=ALU.add)
+
+        def stage_P_pe(j):
+            banks = []
+            for h in range(2):
+                pv = psum.tile([P, 512], F32, name="pv%d" % h)
+                for m in range(3):
+                    for c in range(2):
+                        nc.tensor.matmul(
+                            out=pv[:, 128 * m:128 * m + 128], lhsT=ub[j][:, 1 + 2 * m + c, :],
+                            rhs=w1[:, c, 128 * h:128 * h + 128], start=(c == 0), stop=(c == 1))
+                banks.append(pv)
+            for h in range(2):
+                pt = psum.tile([P, 512], F32, name="pt%d" % h)
+                for m in range(5):
+                    lhsT = ua[j][:, m, :] if m < 4 else ub[j][:, 0, :]
+                    nc.tensor.matmul(
+                        out=pt[:, 64 * m:64 * m + 64], lhsT=lhsT,
+                        rhs=w2[:, 64 * h:64 * h + 64], start=True, stop=True)
+                banks.append(pt)
+            return banks
+
+        def gate_v(j, banks, h):
+            o = osb[j]
+            nc.vector.scalar_tensor_tensor(
+                out=o[:, 512 + 384 * h:896 + 384 * h].rearrange("p (o m) -> p o m", m=3),
+                in0=banks[h][:, 0:384].rearrange("p (m o) -> p o m", m=3),
+                scalar=C1,
+                in1=gates[j][:, 128 * h:128 * h + 128].unsqueeze(2).to_broadcast([P, 128, 3]),
+                op0=ALU.mult, op1=ALU.mult)
+
+        def gate_t(j, banks, h):
+            o = osb[j]
+            nc.vector.scalar_tensor_tensor(
+                out=o[:, 1280 + 320 * h:1600 + 320 * h].rearrange("p (o m) -> p o m", m=5),
+                in0=banks[2 + h][:, 0:320].rearrange("p (m o) -> p o m", m=5),
+                scalar=C2,
+                in1=gates[j][:, 256 + 64 * h:320 + 64 * h].unsqueeze(2).to_broadcast([P, 64, 5]),
+                op0=ALU.mult, op1=ALU.mult)
+
+        def store(j):
+            nc.sync.dma_start(out=ov[:, j, :], in_=osb[j][:])
+
+        for j in range(NT):
+            if j not in STRIDED:
+                deint(j)
+        stage_T(0)
+        regroup(nc.vector.tensor_copy, 0, 512)
+        regroup(nc.scalar.copy, 512, 768)
+        regroup(nc.vector.tensor_copy, 768, 896)
+        quant_w(0, 512)
+        quant_w(768, 896)
+        quant_w(512, 768)
+        b0 = stage_P_pe(0)
+        stage_T(1)
+        pa = stage_M(0)
+        gate_v(0, b0, 0)
+        gate_v(0, b0, 1)
+        combine(0, pa)
+        gate_t(0, b0, 0)
+        gate_t(0, b0, 1)
+        store(0)
+        stage_T(2)
+        pa = stage_M(1)
+        combine(1, pa)
+        for j in range(1, NT):
+            b = stage_P_pe(j)
+            gate_v(j, b, 0)
+            gate_v(j, b, 1)
+            gate_t(j, b, 0)
+            gate_t(j, b, 1)
+            store(j)
+            if j + 1 < NT:
+                pa = stage_M(j + 1)
+                combine(j + 1, pa)
+            if j + 2 < NT:
+                stage_T(j + 2)

@@ -1,9 +1,7 @@
 import math
 from contextlib import ExitStack
 
-import concourse.bass as bass
 import concourse.mybir as mybir
-import concourse.tile as tile
 from concourse.masks import make_identity
 
 BF16 = mybir.dt.bfloat16
@@ -19,8 +17,10 @@ NT = 8
 D = 1920
 FLOPS = 2 * 1024 * (512 * 896 + 3 * 256 * 256 + 5 * 128 * 128)
 
-PIN = True
 STRIDED = (0, 1)
+GADD = ()
+A_SPLIT = 320
+ORDER = [("L", 0), ("L", 100), ("L", 1), ("L", 101), ("L", 102), ("L", 2), ("L", 3), ("L", 4), ("L", 5), ("L", 6), ("L", 7), ("ID", 0), ("Dt", 2), ("Dv", 2), ("Dt", 3), ("Dv", 3), ("Dt", 4), ("Dv", 4), ("Dt", 5), ("Dv", 5), ("Dt", 6), ("Dv", 6), ("Dt", 7), ("Dv", 7), ("T", 0), ("Xs", 0), ("Xa", 0), ("Xb", 0), ("RgBC", 0), ("Q", 0), ("QB", 0), ("T", 1), ("Xs", 1), ("RgA2", 0), ("RgA1", 0), ("QA", 0), ("Q", 1), ("Mb", 0), ("Sg", 0), ("Xa", 1), ("Xb", 1), ("Pv", 0), ("Pt", 0), ("Gv", 0), ("Gt", 0), ("Ma", 0), ("Re", 0), ("C", 0), ("St", 0), ("Mb", 1), ("Sg", 1), ("T", 2), ("Xs", 2), ("Xa", 2), ("Xb", 2), ("Q", 2), ("Ma", 1), ("Re", 1), ("C", 1), ("Pv", 1), ("Gv", 1), ("Pt", 1), ("Gt", 1), ("St", 1), ("Mb", 2), ("Sg", 2), ("Ma", 2), ("Re", 2), ("C", 2), ("T", 3), ("Xs", 3), ("Xa", 3), ("Xb", 3), ("Q", 3), ("Pv", 2), ("Gv", 2), ("Pt", 2), ("Gt", 2), ("St", 2), ("Mb", 3), ("Sg", 3), ("Ma", 3), ("Re", 3), ("C", 3), ("T", 4), ("Xs", 4), ("Xa", 4), ("Xb", 4), ("Q", 4), ("Pv", 3), ("Gv", 3), ("Pt", 3), ("Gt", 3), ("St", 3), ("Mb", 4), ("Sg", 4), ("Ma", 4), ("Re", 4), ("C", 4), ("T", 5), ("Xs", 5), ("Xa", 5), ("Xb", 5), ("Q", 5), ("Pv", 4), ("Gv", 4), ("Pt", 4), ("Gt", 4), ("St", 4), ("Mb", 5), ("Sg", 5), ("Ma", 5), ("Re", 5), ("C", 5), ("T", 6), ("Xs", 6), ("Xa", 6), ("Xb", 6), ("Q", 6), ("Pv", 5), ("Gv", 5), ("Pt", 5), ("Gt", 5), ("St", 5), ("Mb", 6), ("Sg", 6), ("Ma", 6), ("Re", 6), ("C", 6), ("SS", 6), ("T", 7), ("Xs", 7), ("Xa", 7), ("Xb", 7), ("Q", 7), ("Pv", 6), ("Gv", 6), ("SV", 6), ("Pt", 6), ("Gt", 6), ("ST", 6), ("Mb", 7), ("Sg", 7), ("Ma", 7), ("Re", 7), ("C", 7), ("SS", 7), ("Pv", 7), ("Gv", 7), ("SV", 7), ("Pt", 7), ("Gt", 7), ("ST", 7)]
 
 C0 = 1.0 / math.sqrt(512.0)
 C1 = 1.0 / 16.0
@@ -35,43 +35,50 @@ def tile_equivariantmlpblock_kernel(tc, x, W0, W1, W2, out):
         keep = ctx.enter_context(tc.tile_pool(name="keep", bufs=1))
         work = ctx.enter_context(tc.tile_pool(name="work", bufs=NT))
         psum = ctx.enter_context(tc.psum_pool(name="psum", bufs=1))
-        if PIN:
-            ctx.enter_context(tc.manual_schedule())
+        ctx.enter_context(tc.manual_schedule())
 
         xs = []
         for j in range(NT):
             xj = keep.tile([P, D], BF16, name="x%d" % j, align_bytes=64)
             xs.append(xj)
-        w0raw = keep.tile([P, 4, 896], BF16, name="w0raw", align_bytes=64)
+        w0ra = keep.tile([P, 4, 512], BF16, name="w0ra", align_bytes=64)
+        w0rb = keep.tile([P, 4, 384], BF16, name="w0rb", align_bytes=64)
         w1 = keep.tile([P, 2, 256], BF16, name="w1")
         w2 = keep.tile([P, 128], BF16, name="w2")
-        nc.sync.dma_start(out=xs[0][:], in_=xv[:, 0, :])
-        nc.sync.dma_start(
-            out=w0raw[:].rearrange("p (u e) c -> p u (e c)", u=2),
-            in_=W0.rearrange("(u p e) c -> p u (e c)", u=2, p=P, e=2),
-        )
-        nc.sync.dma_start(out=w1[:], in_=W1.rearrange("(c i) o -> i c o", c=2))
-        nc.sync.dma_start(out=w2[:], in_=W2)
-        for j in range(1, NT):
-            nc.sync.dma_start(out=xs[j][:], in_=xv[:, j, :])
+        w0v = W0.rearrange("(u p e) c -> u p e c", u=2, p=P, e=2)
+
+        def load(what):
+            if what == 100:
+                for u in range(2):
+                    nc.sync.dma_start(out=w0rb[:, 2 * u:2 * u + 2, :], in_=w0v[u, :, :, 512:896])
+            elif what == 101:
+                for u in range(2):
+                    nc.sync.dma_start(out=w0ra[:, 2 * u:2 * u + 2, :], in_=w0v[u, :, :, 0:512])
+            elif what == 102:
+                nc.sync.dma_start(out=w1[:].rearrange("p e o -> p (e o)"), in_=W1.rearrange("(j e) o -> j (e o)", e=2))
+                nc.sync.dma_start(out=w2[:], in_=W2)
+            else:
+                nc.sync.dma_start(out=xs[what][:], in_=xv[:, what, :])
 
         idf = keep.tile([P, P], F32, name="idf")
         idb = keep.tile([P, P], BF16, name="idb")
-        make_identity(nc, idf[:])
-        make_identity(nc, idb[:])
         warm = keep.tile([P, 1], F32, name="warm")
         warm2 = keep.tile([P, 1], F32, name="warm2")
-        nc.vector.memset(warm[:], 0.0)
-        nc.scalar.activation(out=warm2[:], in_=warm[:], func=ACT.Sigmoid)
+
+        def consts(unused):
+            make_identity(nc, idf[:])
+            make_identity(nc, idb[:])
+            nc.vector.memset(warm[:], 0.0)
+            nc.scalar.activation(out=warm2[:], in_=warm[:], func=ACT.Sigmoid)
 
         w0g = keep.tile([P, 896, 4], BF16, name="w0g", align_bytes=64)
         w0c = keep.tile([P, 896], U32, name="w0c", align_bytes=64)
         w0s = keep.tile([P, 896], U8, name="w0s", align_bytes=64)
 
-        def regroup(eng_copy, lo, hi):
-            eng_copy(
+        def regroup(copy_fn, raw, base, lo, hi):
+            copy_fn(
                 out=w0g[:, lo:hi, :].rearrange("p (c i) t -> p c t i", i=4),
-                in_=w0raw[:, :, lo:hi].rearrange("p t (c i) -> p c t i", i=4),
+                in_=raw[:, :, lo - base:hi - base].rearrange("p t (c i) -> p c t i", i=4),
             )
 
         def quant_w(lo, hi):
@@ -81,19 +88,38 @@ def tile_equivariantmlpblock_kernel(tc, x, W0, W1, W2, out):
                 in_=w0g[:, lo:hi, :].rearrange("p c t -> p (c t)"),
             )
 
+        def rg_bc(unused):
+            regroup(nc.vector.tensor_copy, w0rb, 512, 512, 896)
+
+        def rg_a1(unused):
+            regroup(nc.vector.tensor_copy, w0ra, 0, 0, A_SPLIT)
+
+        def rg_a2(unused):
+            regroup(nc.scalar.copy, w0ra, 0, A_SPLIT, 512)
+
+        def q_b(unused):
+            quant_w(512, 768)
+            quant_w(768, 896)
+
+        def q_a(unused):
+            quant_w(0, 512)
+
         vd = {}
         td = {}
 
-        def deint(j):
+        def deint_t(j):
             tdj = work.tile([P, 5, 128], BF16, name="td")
-            vdj = work.tile([P, 3, 256], BF16, name="vd")
             nc.gpsimd.tensor_scalar(
                 out=tdj[:], in0=xs[j][:, 1280:1920].rearrange("p (i m) -> p m i", m=5),
                 scalar1=1.0, scalar2=0.0, op0=ALU.mult, op1=ALU.add)
-            nc.gpsimd.tensor_scalar(
-                out=vdj[:], in0=xs[j][:, 512:1280].rearrange("p (i m) -> p m i", m=3),
-                scalar1=1.0, scalar2=0.0, op0=ALU.mult, op1=ALU.add)
             td[j] = tdj
+
+        def deint_v(j):
+            vdj = work.tile([P, 768], BF16, name="vd")
+            nc.gpsimd.tensor_scalar(
+                out=vdj[:].rearrange("p (r j e) -> p r j e", r=3, e=2),
+                in0=xs[j][:, 512:1280].rearrange("p (j r e) -> p r j e", r=3, e=2),
+                scalar1=1.0, scalar2=0.0, op0=ALU.mult, op1=ALU.add)
             vd[j] = vdj
 
         def t_src(j, m):
@@ -101,46 +127,59 @@ def tile_equivariantmlpblock_kernel(tc, x, W0, W1, W2, out):
                 return xs[j][:, 1280:1920].rearrange("p (i m) -> p m i", m=5)[:, m, :]
             return td[j][:, m, :]
 
-        def v_src(j, m, c):
+        def v_src(j, r):
             if j in STRIDED:
-                return xs[j][:, 512:1280].rearrange("p (i m) -> p m i", m=3)[:, m, 128 * c:128 * c + 128]
-            return vd[j][:, m, 128 * c:128 * c + 128]
+                return xs[j][:, 512:1280].bitcast(F32).rearrange("p (j r) -> p r j", r=3)[:, r, :]
+            return vd[j][:].bitcast(F32)[:, 128 * r:128 * r + 128]
 
+        tb = {}
         ua = {}
         ub = {}
+        gs = {}
         sc = {}
         ss = {}
         gates = {}
         osb = {}
+        pab = {}
+        pbb = {}
+        pvb = {}
+        ptb = {}
 
-        def stage_T(j):
-            t1 = psum.tile([P, 1024], BF16, name="t1")
-            t2 = psum.tile([P, 1024], BF16, name="t2")
-            t1f = t1[:, 0:512].bitcast(F32)
+        def st_T(j):
+            t1 = psum.tile([P, 512], F32, name="t1")
+            t2 = psum.tile([P, 512], F32, name="t2")
             xw = xs[j][:, 0:512].bitcast(F32)
             for u in range(2):
-                nc.tensor.transpose(t1f[:, 128 * u:128 * u + 128], xw[:, 128 * u:128 * u + 128], idf[:])
+                nc.tensor.transpose(t1[:, 128 * u:128 * u + 128], xw[:, 128 * u:128 * u + 128], idf[:])
             for m in range(4):
-                nc.tensor.transpose(t1[:, 512 + 128 * m:640 + 128 * m], t_src(j, m), idb[:])
-            nc.tensor.transpose(t2[:, 0:128], t_src(j, 4), idb[:])
-            for m in range(3):
-                for c in range(2):
-                    q = 1 + 2 * m + c
-                    nc.tensor.transpose(t2[:, 128 * q:128 * q + 128], v_src(j, m, c), idb[:])
-            gs = work.tile([P, 512], BF16, name="gs", align_bytes=64)
+                nc.tensor.transpose(t1[:, 256 + 64 * m:320 + 64 * m].bitcast(BF16), t_src(j, m), idb[:])
+            nc.tensor.transpose(t2[:, 384:448].bitcast(BF16), t_src(j, 4), idb[:])
+            for r in range(3):
+                nc.tensor.transpose(t2[:, 128 * r:128 * r + 128], v_src(j, r), idf[:])
+            tb[j] = (t1, t2)
+
+        def st_Xs(j):
+            g = work.tile([P, 512], BF16, name="gs", align_bytes=64)
             nc.scalar.copy(
-                out=gs[:].bitcast(F32).rearrange("p (n u) -> p n u", u=2),
-                in_=t1f.rearrange("p (u n) -> p n u", u=2),
+                out=g[:].bitcast(F32).rearrange("p (n u) -> p n u", u=2),
+                in_=tb[j][0][:, 0:256].rearrange("p (u n) -> p n u", u=2),
             )
-            uaj = work.tile([P, 4, 128], BF16, name="ua")
-            ubj = work.tile([P, 7, 128], BF16, name="ub")
-            nc.scalar.copy(out=uaj[:].rearrange("p a n -> p (a n)"), in_=t1[:, 512:1024])
-            nc.scalar.copy(out=ubj[:].rearrange("p a n -> p (a n)"), in_=t2[:, 0:896])
+            gs[j] = g
+
+        def st_Xa(j):
+            uaj = work.tile([P, 512], BF16, name="ua")
+            nc.scalar.copy(out=uaj[:].bitcast(F32), in_=tb[j][0][:, 256:512])
+            ua[j] = uaj
+
+        def st_Xb(j):
+            ubj = work.tile([P, 896], BF16, name="ub")
+            nc.scalar.copy(out=ubj[:].bitcast(F32), in_=tb[j][1][:, 0:448])
+            ub[j] = ubj
+
+        def st_Q(j):
             scj = work.tile([P, 128], U32, name="sc", align_bytes=64)
             ssj = work.tile([P, 128], U8, name="ss", align_bytes=64)
-            nc.vector.quantize_mx(out=scj[:].bitcast(FP8X4), scales=ssj[:], in_=gs[:])
-            ua[j] = uaj
-            ub[j] = ubj
+            nc.vector.quantize_mx(out=scj[:].bitcast(FP8X4), scales=ssj[:], in_=gs[j][:])
             sc[j] = scj
             ss[j] = ssj
 
@@ -150,98 +189,101 @@ def tile_equivariantmlpblock_kernel(tc, x, W0, W1, W2, out):
                 rhs=w0c[:, lo:hi].bitcast(FP8X4), rhs_scale=w0s[:, lo:hi],
                 start=True, stop=True)
 
-        def stage_M(j):
+        def st_Mb(j):
             pb = psum.tile([P, 512], F32, name="pb")
-            pa = psum.tile([P, 512], F32, name="pa")
             mx(j, pb[:, 0:256], 512, 768)
             mx(j, pb[:, 256:384], 768, 896)
-            mx(j, pa[:], 0, 512)
-            g = work.tile([P, 384], F32, name="g")
-            o = work.tile([P, D], F32, name="o")
-            nc.scalar.activation(out=g[:], in_=pb[:, 0:384], func=ACT.Sigmoid, scale=C0)
-            nc.scalar.activation(out=o[:, 0:512], in_=pa[:], func=ACT.Relu, scale=0.99 * C0)
-            gates[j] = g
-            osb[j] = o
-            return pa
+            pbb[j] = pb
 
-        def combine(j, pa):
-            o = osb[j]
+        def st_Sg(j):
+            g = work.tile([P, 384], F32, name="g")
+            nc.scalar.activation(out=g[:], in_=pbb[j][:, 0:384], func=ACT.Sigmoid, scale=C0)
+            gates[j] = g
+
+        def get_o(j):
+            if j not in osb:
+                o = work.tile([P, D], F32, name="o")
+                osb[j] = o
+            return osb[j]
+
+        def st_Ma(j):
+            pa = psum.tile([P, 512], F32, name="pa")
+            mx(j, pa[:], 0, 512)
+            pab[j] = pa
+
+        def st_Re(j):
+            o = get_o(j)
+            nc.scalar.activation(out=o[:, 0:512], in_=pab[j][:], func=ACT.Relu, scale=0.99 * C0)
+
+        def st_C(j):
+            o = get_o(j)
             nc.vector.scalar_tensor_tensor(
-                out=o[:, 0:512], in0=pa[:], scalar=0.01 * C0, in1=o[:, 0:512],
+                out=o[:, 0:512], in0=pab[j][:], scalar=0.01 * C0, in1=o[:, 0:512],
                 op0=ALU.mult, op1=ALU.add)
 
-        def stage_P_pe(j):
+        def st_Pv(j):
+            uv = ub[j][:, 0:768].rearrange("p (r n e) -> p r n e", r=3, e=2)
             banks = []
             for h in range(2):
                 pv = psum.tile([P, 512], F32, name="pv%d" % h)
                 for m in range(3):
-                    for c in range(2):
+                    for par in range(2):
+                        k = 3 * par + m
                         nc.tensor.matmul(
-                            out=pv[:, 128 * m:128 * m + 128], lhsT=ub[j][:, 1 + 2 * m + c, :],
-                            rhs=w1[:, c, 128 * h:128 * h + 128], start=(c == 0), stop=(c == 1))
+                            out=pv[:, 128 * m:128 * m + 128], lhsT=uv[:, k // 2, :, k % 2],
+                            rhs=w1[:, par, 128 * h:128 * h + 128], start=(par == 0), stop=(par == 1))
                 banks.append(pv)
+            pvb[j] = banks
+
+        def st_Pt(j):
+            banks = []
             for h in range(2):
                 pt = psum.tile([P, 512], F32, name="pt%d" % h)
                 for m in range(5):
-                    lhsT = ua[j][:, m, :] if m < 4 else ub[j][:, 0, :]
+                    lhsT = ua[j][:, 128 * m:128 * m + 128] if m < 4 else ub[j][:, 768:896]
                     nc.tensor.matmul(
                         out=pt[:, 64 * m:64 * m + 64], lhsT=lhsT,
                         rhs=w2[:, 64 * h:64 * h + 64], start=True, stop=True)
                 banks.append(pt)
-            return banks
+            ptb[j] = banks
 
-        def gate_v(j, banks, h):
-            o = osb[j]
-            nc.vector.scalar_tensor_tensor(
-                out=o[:, 512 + 384 * h:896 + 384 * h].rearrange("p (o m) -> p o m", m=3),
-                in0=banks[h][:, 0:384].rearrange("p (m o) -> p o m", m=3),
-                scalar=C1,
-                in1=gates[j][:, 128 * h:128 * h + 128].unsqueeze(2).to_broadcast([P, 128, 3]),
-                op0=ALU.mult, op1=ALU.mult)
+        def st_Gv(j):
+            o = get_o(j)
+            for h in range(2):
+                nc.vector.scalar_tensor_tensor(
+                    out=o[:, 512 + 384 * h:896 + 384 * h].rearrange("p (o m) -> p o m", m=3),
+                    in0=pvb[j][h][:, 0:384].rearrange("p (m o) -> p o m", m=3),
+                    scalar=C1,
+                    in1=gates[j][:, 128 * h:128 * h + 128].unsqueeze(2).to_broadcast([P, 128, 3]),
+                    op0=ALU.mult, op1=ALU.mult)
 
-        def gate_t(j, banks, h):
-            o = osb[j]
-            nc.vector.scalar_tensor_tensor(
-                out=o[:, 1280 + 320 * h:1600 + 320 * h].rearrange("p (o m) -> p o m", m=5),
-                in0=banks[2 + h][:, 0:320].rearrange("p (m o) -> p o m", m=5),
-                scalar=C2,
-                in1=gates[j][:, 256 + 64 * h:320 + 64 * h].unsqueeze(2).to_broadcast([P, 64, 5]),
-                op0=ALU.mult, op1=ALU.mult)
+        def st_Gt(j):
+            o = get_o(j)
+            for h in range(2):
+                nc.vector.scalar_tensor_tensor(
+                    out=o[:, 1280 + 320 * h:1600 + 320 * h].rearrange("p (o m) -> p o m", m=5),
+                    in0=ptb[j][h][:, 0:320].rearrange("p (m o) -> p o m", m=5),
+                    scalar=C2,
+                    in1=gates[j][:, 256 + 64 * h:320 + 64 * h].unsqueeze(2).to_broadcast([P, 64, 5]),
+                    op0=ALU.mult, op1=ALU.mult)
 
-        def store(j):
+        def st_St(j):
             nc.sync.dma_start(out=ov[:, j, :], in_=osb[j][:])
 
-        for j in range(NT):
-            if j not in STRIDED:
-                deint(j)
-        stage_T(0)
-        regroup(nc.vector.tensor_copy, 0, 512)
-        regroup(nc.scalar.copy, 512, 768)
-        regroup(nc.vector.tensor_copy, 768, 896)
-        quant_w(0, 512)
-        quant_w(768, 896)
-        quant_w(512, 768)
-        b0 = stage_P_pe(0)
-        stage_T(1)
-        pa = stage_M(0)
-        gate_v(0, b0, 0)
-        gate_v(0, b0, 1)
-        combine(0, pa)
-        gate_t(0, b0, 0)
-        gate_t(0, b0, 1)
-        store(0)
-        stage_T(2)
-        pa = stage_M(1)
-        combine(1, pa)
-        for j in range(1, NT):
-            b = stage_P_pe(j)
-            gate_v(j, b, 0)
-            gate_v(j, b, 1)
-            gate_t(j, b, 0)
-            gate_t(j, b, 1)
-            store(j)
-            if j + 1 < NT:
-                pa = stage_M(j + 1)
-                combine(j + 1, pa)
-            if j + 2 < NT:
-                stage_T(j + 2)
+        def st_SS(j):
+            nc.sync.dma_start(out=ov[:, j, 0:512], in_=osb[j][:, 0:512])
+
+        def st_SV(j):
+            nc.sync.dma_start(out=ov[:, j, 512:1280], in_=osb[j][:, 512:1280])
+
+        def st_ST(j):
+            nc.sync.dma_start(out=ov[:, j, 1280:1920], in_=osb[j][:, 1280:1920])
+
+        funcs = {
+            "L": load, "ID": consts, "RgBC": rg_bc, "RgA1": rg_a1, "RgA2": rg_a2, "QB": q_b, "QA": q_a,
+            "Dt": deint_t, "Dv": deint_v, "T": st_T, "Xs": st_Xs, "Xa": st_Xa, "Xb": st_Xb, "Q": st_Q,
+            "Mb": st_Mb, "Sg": st_Sg, "Ma": st_Ma, "Re": st_Re, "C": st_C, "Pv": st_Pv, "Pt": st_Pt,
+            "Gv": st_Gv, "Gt": st_Gt, "St": st_St, "SS": st_SS, "SV": st_SV, "ST": st_ST,
+        }
+        for name, j in ORDER:
+            funcs[name](j)

@@ -230,7 +230,7 @@ def tile_equivariantmlpblock_kernel(tc, x, W0, W1, W2, out):
                     for par in range(2):
                         k = 3 * par + m
                         nc.tensor.matmul(
-                            out=pv[:, 128 * m:128 * m + 128], lhsT=uv[:, k // 2, :, k % 2],
+                            out=pv[:, 0:384].rearrange("p (o m) -> p m o", m=3)[:, m, :], lhsT=uv[:, k // 2, :, k % 2],
                             rhs=w1[:, par, 128 * h:128 * h + 128], start=(par == 0), stop=(par == 1))
                 banks.append(pv)
             pvb[j] = banks
@@ -242,7 +242,7 @@ def tile_equivariantmlpblock_kernel(tc, x, W0, W1, W2, out):
                 for m in range(5):
                     lhsT = ua[j][:, 128 * m:128 * m + 128] if m < 4 else ub[j][:, 768:896]
                     nc.tensor.matmul(
-                        out=pt[:, 64 * m:64 * m + 64], lhsT=lhsT,
+                        out=pt[:, 0:320].rearrange("p (o m) -> p m o", m=5)[:, m, :], lhsT=lhsT,
                         rhs=w2[:, 64 * h:64 * h + 64], start=True, stop=True)
                 banks.append(pt)
             ptb[j] = banks
@@ -252,7 +252,7 @@ def tile_equivariantmlpblock_kernel(tc, x, W0, W1, W2, out):
             for h in range(2):
                 nc.vector.scalar_tensor_tensor(
                     out=o[:, 512 + 384 * h:896 + 384 * h].rearrange("p (o m) -> p o m", m=3),
-                    in0=pvb[j][h][:, 0:384].rearrange("p (m o) -> p o m", m=3),
+                    in0=pvb[j][h][:, 0:384].rearrange("p (o m) -> p o m", m=3),
                     scalar=C1,
                     in1=gates[j][:, 128 * h:128 * h + 128].unsqueeze(2).to_broadcast([P, 128, 3]),
                     op0=ALU.mult, op1=ALU.mult)
@@ -262,7 +262,7 @@ def tile_equivariantmlpblock_kernel(tc, x, W0, W1, W2, out):
             for h in range(2):
                 nc.vector.scalar_tensor_tensor(
                     out=o[:, 1280 + 320 * h:1600 + 320 * h].rearrange("p (o m) -> p o m", m=5),
-                    in0=ptb[j][h][:, 0:320].rearrange("p (m o) -> p o m", m=5),
+                    in0=ptb[j][h][:, 0:320].rearrange("p (o m) -> p o m", m=5),
                     scalar=C2,
                     in1=gates[j][:, 256 + 64 * h:320 + 64 * h].unsqueeze(2).to_broadcast([P, 64, 5]),
                     op0=ALU.mult, op1=ALU.mult)

@@ -17,10 +17,10 @@ NT = 8
 D = 1920
 FLOPS = 2 * 1024 * (512 * 896 + 3 * 256 * 256 + 5 * 128 * 128)
 
-STRIDED = (0, 1)
+STRIDED = (0,)
 GADD = ()
 A_SPLIT = 320
-ORDER = [("L", 0), ("L", 100), ("L", 1), ("L", 101), ("L", 102), ("L", 2), ("L", 3), ("L", 4), ("L", 5), ("L", 6), ("L", 7), ("ID", 0), ("Dt", 2), ("Dv", 2), ("Dt", 3), ("Dv", 3), ("Dt", 4), ("Dv", 4), ("Dt", 5), ("Dv", 5), ("Dt", 6), ("Dv", 6), ("Dt", 7), ("Dv", 7), ("T", 0), ("Xs", 0), ("Xa", 0), ("Xb", 0), ("RgBC", 0), ("Q", 0), ("QB", 0), ("T", 1), ("Xs", 1), ("RgA2", 0), ("RgA1", 0), ("QA", 0), ("Q", 1), ("Mb", 0), ("Sg", 0), ("Xa", 1), ("Xb", 1), ("Pv", 0), ("Pt", 0), ("Gv", 0), ("Gt", 0), ("Ma", 0), ("Re", 0), ("C", 0), ("St", 0), ("Mb", 1), ("Sg", 1), ("T", 2), ("Xs", 2), ("Xa", 2), ("Xb", 2), ("Q", 2), ("Ma", 1), ("Re", 1), ("C", 1), ("Pv", 1), ("Gv", 1), ("Pt", 1), ("Gt", 1), ("St", 1), ("Mb", 2), ("Sg", 2), ("Ma", 2), ("Re", 2), ("C", 2), ("T", 3), ("Xs", 3), ("Xa", 3), ("Xb", 3), ("Q", 3), ("Pv", 2), ("Gv", 2), ("Pt", 2), ("Gt", 2), ("St", 2), ("Mb", 3), ("Sg", 3), ("Ma", 3), ("Re", 3), ("C", 3), ("T", 4), ("Xs", 4), ("Xa", 4), ("Xb", 4), ("Q", 4), ("Pv", 3), ("Gv", 3), ("Pt", 3), ("Gt", 3), ("St", 3), ("Mb", 4), ("Sg", 4), ("Ma", 4), ("Re", 4), ("C", 4), ("T", 5), ("Xs", 5), ("Xa", 5), ("Xb", 5), ("Q", 5), ("Pv", 4), ("Gv", 4), ("Pt", 4), ("Gt", 4), ("St", 4), ("Mb", 5), ("Sg", 5), ("Ma", 5), ("Re", 5), ("C", 5), ("T", 6), ("Xs", 6), ("Xa", 6), ("Xb", 6), ("Q", 6), ("Pv", 5), ("Gv", 5), ("Pt", 5), ("Gt", 5), ("St", 5), ("Mb", 6), ("Sg", 6), ("Ma", 6), ("Re", 6), ("C", 6), ("SS", 6), ("T", 7), ("Xs", 7), ("Xa", 7), ("Xb", 7), ("Q", 7), ("Pv", 6), ("Gv", 6), ("SV", 6), ("Pt", 6), ("Gt", 6), ("ST", 6), ("Mb", 7), ("Sg", 7), ("Ma", 7), ("Re", 7), ("C", 7), ("SS", 7), ("Pv", 7), ("Gv", 7), ("SV", 7), ("Pt", 7), ("Gt", 7), ("ST", 7)]
+ORDER = [("L", 0), ("L", 100), ("L", 1), ("L", 101), ("L", 102), ("L", 2), ("L", 3), ("L", 4), ("L", 5), ("L", 6), ("L", 7), ("ID", 0), ("Dt", 1), ("Dv", 1), ("Dt", 2), ("Dv", 2), ("Dt", 3), ("Dv", 3), ("Dt", 4), ("Dv", 4), ("Dt", 5), ("Dv", 5), ("Dt", 6), ("Dv", 6), ("Dt", 7), ("Dv", 7), ("T", 0), ("Xs", 0), ("Xa", 0), ("Xb", 0), ("RgBC", 0), ("Q", 0), ("QB", 0), ("RgA2", 0), ("RgA1", 0), ("QA", 0), ("Mb", 0), ("Sg", 0), ("Pt", 0), ("Gt", 0), ("T", 1), ("Xs", 1), ("Q", 1), ("Xa", 1), ("Xb", 1), ("Pv", 0), ("Gv", 0), ("Ma", 0), ("Re", 0), ("C", 0), ("St", 0), ("Mb", 1), ("Sg", 1), ("Pt", 1), ("Gt", 1), ("T", 2), ("Xs", 2), ("Q", 2), ("Xa", 2), ("Xb", 2), ("Pv", 1), ("Gv", 1), ("Ma", 1), ("Re", 1), ("C", 1), ("St", 1), ("Mb", 2), ("Sg", 2), ("Pt", 2), ("Gt", 2), ("T", 3), ("Xs", 3), ("Q", 3), ("Xa", 3), ("Xb", 3), ("Pv", 2), ("Gv", 2), ("Ma", 2), ("Re", 2), ("C", 2), ("St", 2), ("Mb", 3), ("Sg", 3), ("Pt", 3), ("Gt", 3), ("T", 4), ("Xs", 4), ("Q", 4), ("Xa", 4), ("Xb", 4), ("Pv", 3), ("Gv", 3), ("Ma", 3), ("Re", 3), ("C", 3), ("St", 3), ("Mb", 4), ("Sg", 4), ("Pt", 4), ("Gt", 4), ("ST", 4), ("T", 5), ("Xs", 5), ("Q", 5), ("Xa", 5), ("Xb", 5), ("Pv", 4), ("Gv", 4), ("SV", 4), ("Ma", 4), ("Re", 4), ("C", 4), ("SS", 4), ("Mb", 5), ("Sg", 5), ("Pt", 5), ("Gt", 5), ("ST", 5), ("T", 6), ("Xs", 6), ("Q", 6), ("Xa", 6), ("Xb", 6), ("Pv", 5), ("Gv", 5), ("SV", 5), ("Ma", 5), ("Re", 5), ("C", 5), ("SS", 5), ("Mb", 6), ("Sg", 6), ("Pt", 6), ("Gt", 6), ("ST", 6), ("T", 7), ("Xs", 7), ("Q", 7), ("Xa", 7), ("Xb", 7), ("Pv", 6), ("Gv", 6), ("SV", 6), ("Ma", 6), ("Re", 6), ("C", 6), ("SS", 6), ("Mb", 7), ("Sg", 7), ("Pt", 7), ("Gt", 7), ("ST", 7), ("Pv", 7), ("Gv", 7), ("SV", 7), ("Ma", 7), ("Re", 7), ("C", 7), ("SS", 7)]
 
 C0 = 1.0 / math.sqrt(512.0)
 C1 = 1.0 / 16.0
@@ -230,7 +230,7 @@ def tile_equivariantmlpblock_kernel(tc, x, W0, W1, W2, out):
                     for par in range(2):
                         k = 3 * par + m
                         nc.tensor.matmul(
-                            out=pv[:, 0:384].rearrange("p (o m) -> p m o", m=3)[:, m, :], lhsT=uv[:, k // 2, :, k % 2],
+                            out=pv[:, 128 * m:128 * m + 128], lhsT=uv[:, k // 2, :, k % 2],
                             rhs=w1[:, par, 128 * h:128 * h + 128], start=(par == 0), stop=(par == 1))
                 banks.append(pv)
             pvb[j] = banks
@@ -242,7 +242,7 @@ def tile_equivariantmlpblock_kernel(tc, x, W0, W1, W2, out):
                 for m in range(5):
                     lhsT = ua[j][:, 128 * m:128 * m + 128] if m < 4 else ub[j][:, 768:896]
                     nc.tensor.matmul(
-                        out=pt[:, 0:320].rearrange("p (o m) -> p m o", m=5)[:, m, :], lhsT=lhsT,
+                        out=pt[:, 64 * m:64 * m + 64], lhsT=lhsT,
                         rhs=w2[:, 64 * h:64 * h + 64], start=True, stop=True)
                 banks.append(pt)
             ptb[j] = banks
@@ -252,7 +252,7 @@ def tile_equivariantmlpblock_kernel(tc, x, W0, W1, W2, out):
             for h in range(2):
                 nc.vector.scalar_tensor_tensor(
                     out=o[:, 512 + 384 * h:896 + 384 * h].rearrange("p (o m) -> p o m", m=3),
-                    in0=pvb[j][h][:, 0:384].rearrange("p (o m) -> p o m", m=3),
+                    in0=pvb[j][h][:, 0:384].rearrange("p (m o) -> p o m", m=3),
                     scalar=C1,
                     in1=gates[j][:, 128 * h:128 * h + 128].unsqueeze(2).to_broadcast([P, 128, 3]),
                     op0=ALU.mult, op1=ALU.mult)
@@ -262,7 +262,7 @@ def tile_equivariantmlpblock_kernel(tc, x, W0, W1, W2, out):
             for h in range(2):
                 nc.vector.scalar_tensor_tensor(
                     out=o[:, 1280 + 320 * h:1600 + 320 * h].rearrange("p (o m) -> p o m", m=5),
-                    in0=ptb[j][h][:, 0:320].rearrange("p (o m) -> p o m", m=5),
+                    in0=ptb[j][h][:, 0:320].rearrange("p (m o) -> p o m", m=5),
                     scalar=C2,
                     in1=gates[j][:, 256 + 64 * h:320 + 64 * h].unsqueeze(2).to_broadcast([P, 64, 5]),
                     op0=ALU.mult, op1=ALU.mult)

@@ -17,10 +17,11 @@ NT = 8
 D = 1920
 FLOPS = 2 * 1024 * (512 * 896 + 3 * 256 * 256 + 5 * 128 * 128)
 
+STRIDED_V = (0, 1, 2, 3, 4, 5, 6, 7)
 STRIDED = (0,)
 GADD = ()
 A_SPLIT = 320
-ORDER = [("L", 0), ("L", 100), ("L", 1), ("L", 101), ("L", 102), ("L", 2), ("L", 3), ("L", 4), ("L", 5), ("L", 6), ("L", 7), ("ID", 0), ("Dt", 1), ("Dv", 1), ("Dt", 2), ("Dv", 2), ("Dt", 3), ("Dv", 3), ("Dt", 4), ("Dv", 4), ("Dt", 5), ("Dv", 5), ("Dt", 6), ("Dv", 6), ("Dt", 7), ("Dv", 7), ("T", 0), ("Xs", 0), ("Xa", 0), ("Xb", 0), ("RgBC", 0), ("Q", 0), ("QB", 0), ("RgA2", 0), ("RgA1", 0), ("QA", 0), ("Mb", 0), ("Sg", 0), ("Pt", 0), ("Gt", 0), ("T", 1), ("Xs", 1), ("Q", 1), ("Xa", 1), ("Xb", 1), ("Pv", 0), ("Gv", 0), ("Ma", 0), ("Re", 0), ("C", 0), ("St", 0), ("Mb", 1), ("Sg", 1), ("Pt", 1), ("Gt", 1), ("T", 2), ("Xs", 2), ("Q", 2), ("Xa", 2), ("Xb", 2), ("Pv", 1), ("Gv", 1), ("Ma", 1), ("Re", 1), ("C", 1), ("St", 1), ("Mb", 2), ("Sg", 2), ("Pt", 2), ("Gt", 2), ("T", 3), ("Xs", 3), ("Q", 3), ("Xa", 3), ("Xb", 3), ("Pv", 2), ("Gv", 2), ("Ma", 2), ("Re", 2), ("C", 2), ("St", 2), ("Mb", 3), ("Sg", 3), ("Pt", 3), ("Gt", 3), ("T", 4), ("Xs", 4), ("Q", 4), ("Xa", 4), ("Xb", 4), ("Pv", 3), ("Gv", 3), ("Ma", 3), ("Re", 3), ("C", 3), ("St", 3), ("Mb", 4), ("Sg", 4), ("Pt", 4), ("Gt", 4), ("ST", 4), ("T", 5), ("Xs", 5), ("Q", 5), ("Xa", 5), ("Xb", 5), ("Pv", 4), ("Gv", 4), ("SV", 4), ("Ma", 4), ("Re", 4), ("C", 4), ("SS", 4), ("Mb", 5), ("Sg", 5), ("Pt", 5), ("Gt", 5), ("ST", 5), ("T", 6), ("Xs", 6), ("Q", 6), ("Xa", 6), ("Xb", 6), ("Pv", 5), ("Gv", 5), ("SV", 5), ("Ma", 5), ("Re", 5), ("C", 5), ("SS", 5), ("Mb", 6), ("Sg", 6), ("Pt", 6), ("Gt", 6), ("ST", 6), ("T", 7), ("Xs", 7), ("Q", 7), ("Xa", 7), ("Xb", 7), ("Pv", 6), ("Gv", 6), ("SV", 6), ("Ma", 6), ("Re", 6), ("C", 6), ("SS", 6), ("Mb", 7), ("Sg", 7), ("Pt", 7), ("Gt", 7), ("ST", 7), ("Pv", 7), ("Gv", 7), ("SV", 7), ("Ma", 7), ("Re", 7), ("C", 7), ("SS", 7)]
+ORDER = [("L", 0), ("L", 100), ("L", 1), ("L", 101), ("L", 102), ("L", 2), ("L", 3), ("L", 4), ("L", 5), ("L", 6), ("L", 7), ("ID", 0), ("Dt", 1), ("Dt", 2), ("Dt", 3), ("Dt", 4), ("Dt", 5), ("Dt", 6), ("Dt", 7), ("T", 0), ("Xs", 0), ("Xa", 0), ("Xb", 0), ("RgBC", 0), ("Q", 0), ("QB", 0), ("RgA2", 0), ("RgA1", 0), ("QA", 0), ("Mb", 0), ("Sg", 0), ("Pt", 0), ("Gt", 0), ("T", 1), ("Xs", 1), ("Q", 1), ("Xa", 1), ("Xb", 1), ("Pv", 0), ("Gv", 0), ("Ma", 0), ("Re", 0), ("C", 0), ("St", 0), ("Mb", 1), ("Sg", 1), ("Pt", 1), ("Gt", 1), ("T", 2), ("Xs", 2), ("Q", 2), ("Xa", 2), ("Xb", 2), ("Pv", 1), ("Gv", 1), ("Ma", 1), ("Re", 1), ("C", 1), ("St", 1), ("Mb", 2), ("Sg", 2), ("Pt", 2), ("Gt", 2), ("T", 3), ("Xs", 3), ("Q", 3), ("Xa", 3), ("Xb", 3), ("Pv", 2), ("Gv", 2), ("Ma", 2), ("Re", 2), ("C", 2), ("St", 2), ("Mb", 3), ("Sg", 3), ("Pt", 3), ("Gt", 3), ("T", 4), ("Xs", 4), ("Q", 4), ("Xa", 4), ("Xb", 4), ("Pv", 3), ("Gv", 3), ("Ma", 3), ("Re", 3), ("C", 3), ("St", 3), ("Mb", 4), ("Sg", 4), ("Pt", 4), ("Gt", 4), ("ST", 4), ("T", 5), ("Xs", 5), ("Q", 5), ("Xa", 5), ("Xb", 5), ("Pv", 4), ("Gv", 4), ("SV", 4), ("Ma", 4), ("Re", 4), ("C", 4), ("SS", 4), ("Mb", 5), ("Sg", 5), ("Pt", 5), ("Gt", 5), ("ST", 5), ("T", 6), ("Xs", 6), ("Q", 6), ("Xa", 6), ("Xb", 6), ("Pv", 5), ("Gv", 5), ("SV", 5), ("Ma", 5), ("Re", 5), ("C", 5), ("SS", 5), ("Mb", 6), ("Sg", 6), ("Pt", 6), ("Gt", 6), ("ST", 6), ("T", 7), ("Xs", 7), ("Q", 7), ("Xa", 7), ("Xb", 7), ("Pv", 6), ("Gv", 6), ("SV", 6), ("Ma", 6), ("Re", 6), ("C", 6), ("SS", 6), ("Mb", 7), ("Sg", 7), ("Pt", 7), ("Gt", 7), ("ST", 7), ("Pv", 7), ("Gv", 7), ("SV", 7), ("Ma", 7), ("Re", 7), ("C", 7), ("SS", 7)]
 
 C0 = 1.0 / math.sqrt(512.0)
 C1 = 1.0 / 16.0
@@ -128,7 +129,7 @@ def tile_equivariantmlpblock_kernel(tc, x, W0, W1, W2, out):
             return td[j][:, m, :]
 
         def v_src(j, r):
-            if j in STRIDED:
+            if j in STRIDED_V:
                 return xs[j][:, 512:1280].bitcast(F32).rearrange("p (j r) -> p r j", r=3)[:, r, :]
             return vd[j][:].bitcast(F32)[:, 128 * r:128 * r + 128]
 

@@ -17,11 +17,35 @@ NT = 8
 D = 1920
 FLOPS = 2 * 1024 * (512 * 896 + 3 * 256 * 256 + 5 * 128 * 128)
 
-STRIDED_V = (0, 1, 2, 3, 4, 5, 6, 7)
-STRIDED = (0,)
+STRIDED_V = ()
+STRIDED = ()
 GADD = ()
 A_SPLIT = 320
-ORDER = [("L", 0), ("L", 100), ("L", 1), ("L", 101), ("L", 102), ("L", 2), ("L", 3), ("L", 4), ("L", 5), ("L", 6), ("L", 7), ("ID", 0), ("Dt", 1), ("Dt", 2), ("Dt", 3), ("Dt", 4), ("Dt", 5), ("Dt", 6), ("Dt", 7), ("T", 0), ("Xs", 0), ("Xa", 0), ("Xb", 0), ("RgBC", 0), ("Q", 0), ("QB", 0), ("RgA2", 0), ("RgA1", 0), ("QA", 0), ("Mb", 0), ("Sg", 0), ("Pt", 0), ("Gt", 0), ("T", 1), ("Xs", 1), ("Q", 1), ("Xa", 1), ("Xb", 1), ("Pv", 0), ("Gv", 0), ("Ma", 0), ("Re", 0), ("C", 0), ("St", 0), ("Mb", 1), ("Sg", 1), ("Pt", 1), ("Gt", 1), ("T", 2), ("Xs", 2), ("Q", 2), ("Xa", 2), ("Xb", 2), ("Pv", 1), ("Gv", 1), ("Ma", 1), ("Re", 1), ("C", 1), ("St", 1), ("Mb", 2), ("Sg", 2), ("Pt", 2), ("Gt", 2), ("T", 3), ("Xs", 3), ("Q", 3), ("Xa", 3), ("Xb", 3), ("Pv", 2), ("Gv", 2), ("Ma", 2), ("Re", 2), ("C", 2), ("St", 2), ("Mb", 3), ("Sg", 3), ("Pt", 3), ("Gt", 3), ("T", 4), ("Xs", 4), ("Q", 4), ("Xa", 4), ("Xb", 4), ("Pv", 3), ("Gv", 3), ("Ma", 3), ("Re", 3), ("C", 3), ("St", 3), ("Mb", 4), ("Sg", 4), ("Pt", 4), ("Gt", 4), ("ST", 4), ("T", 5), ("Xs", 5), ("Q", 5), ("Xa", 5), ("Xb", 5), ("Pv", 4), ("Gv", 4), ("SV", 4), ("Ma", 4), ("Re", 4), ("C", 4), ("SS", 4), ("Mb", 5), ("Sg", 5), ("Pt", 5), ("Gt", 5), ("ST", 5), ("T", 6), ("Xs", 6), ("Q", 6), ("Xa", 6), ("Xb", 6), ("Pv", 5), ("Gv", 5), ("SV", 5), ("Ma", 5), ("Re", 5), ("C", 5), ("SS", 5), ("Mb", 6), ("Sg", 6), ("Pt", 6), ("Gt", 6), ("ST", 6), ("T", 7), ("Xs", 7), ("Q", 7), ("Xa", 7), ("Xb", 7), ("Pv", 6), ("Gv", 6), ("SV", 6), ("Ma", 6), ("Re", 6), ("C", 6), ("SS", 6), ("Mb", 7), ("Sg", 7), ("Pt", 7), ("Gt", 7), ("ST", 7), ("Pv", 7), ("Gv", 7), ("SV", 7), ("Ma", 7), ("Re", 7), ("C", 7), ("SS", 7)]
+SPLIT_STORES = (4, 5, 6, 7)
+
+
+def make_order():
+    o = [("L", 0), ("L", 100), ("L", 1), ("L", 101), ("L", 102)]
+    o += [("L", j) for j in range(2, NT)]
+    o += [("ID", 0)]
+    for j in range(NT):
+        o += [("Dt", j), ("Dv", j)]
+    o += [("T", 0), ("Xs", 0), ("Xa", 0), ("Xb", 0), ("RgBC", 0), ("Q", 0), ("QB", 0), ("RgA2", 0), ("RgA1", 0), ("QA", 0)]
+    for j in range(NT):
+        o += [("Mb", j), ("Sg", j), ("Pt", j), ("Gt", j)]
+        if j in SPLIT_STORES:
+            o += [("ST", j)]
+        if j + 1 < NT:
+            o += [("T", j + 1), ("Xs", j + 1), ("Q", j + 1), ("Xa", j + 1), ("Xb", j + 1)]
+        o += [("Pv", j), ("Gv", j)]
+        if j in SPLIT_STORES:
+            o += [("SV", j)]
+        o += [("Ma", j), ("Re", j), ("C", j)]
+        o += [("SS", j)] if j in SPLIT_STORES else [("St", j)]
+    return o
+
+
+ORDER = make_order()
 
 C0 = 1.0 / math.sqrt(512.0)
 C1 = 1.0 / 16.0
@@ -110,17 +134,18 @@ def tile_equivariantmlpblock_kernel(tc, x, W0, W1, W2, out):
 
         def deint_t(j):
             tdj = work.tile([P, 5, 128], BF16, name="td")
-            nc.gpsimd.tensor_scalar(
-                out=tdj[:], in0=xs[j][:, 1280:1920].rearrange("p (i m) -> p m i", m=5),
-                scalar1=1.0, scalar2=0.0, op0=ALU.mult, op1=ALU.add)
+            src = xs[j][:, 1280:1920].rearrange("p (i m) -> p m i", m=5)
+            if j == 0:
+                nc.vector.tensor_copy(out=tdj[:], in_=src)
+            else:
+                nc.gpsimd.tensor_scalar(out=tdj[:], in0=src, scalar1=1.0, scalar2=0.0, op0=ALU.mult, op1=ALU.add)
             td[j] = tdj
 
         def deint_v(j):
             vdj = work.tile([P, 768], BF16, name="vd")
-            nc.gpsimd.tensor_scalar(
-                out=vdj[:].rearrange("p (r j e) -> p r j e", r=3, e=2),
-                in0=xs[j][:, 512:1280].rearrange("p (j r e) -> p r j e", r=3, e=2),
-                scalar1=1.0, scalar2=0.0, op0=ALU.mult, op1=ALU.add)
+            dst = vdj[:].bitcast(F32).rearrange("p (r j) -> p r j", r=3)
+            src = xs[j][:, 512:1280].bitcast(F32).rearrange("p (j r) -> p r j", r=3)
+            (nc.vector if j == 0 else nc.gpsimd).tensor_copy(out=dst, in_=src)
             vd[j] = vdj
 
         def t_src(j, m):

@@ -17,34 +17,36 @@ NT = 8
 D = 1920
 FLOPS = 2 * 1024 * (512 * 896 + 3 * 256 * 256 + 5 * 128 * 128)
 
-STRIDED_V = ()
-STRIDED = ()
+STRIDED_V = (0, 1)
+STRIDED = (0, 1)
 GADD = ()
 A_SPLIT = 320
-SPLIT_STORES = (4, 5, 6, 7)
-
-
 def make_order():
-    o = [("L", 0), ("L", 100), ("L", 1), ("L", 101), ("L", 102)]
-    o += [("L", j) for j in range(2, NT)]
-    o += [("ID", 0)]
+    o = [("L", 0), ("L", 100), ("L", 101), ("L", 102)] + [("L", j) for j in range(1, NT)] + [("ID", 0)]
+    done = set()
+
+    def put(name, j):
+        if j < NT and (name, j) not in done:
+            done.add((name, j))
+            o.append((name, j))
+            if name in STORE_AFTER:
+                o.append((STORE_AFTER[name], j))
+
+    for w in HEAD.split():
+        put(w[:-1], int(w[-1]))
     for j in range(NT):
-        o += [("Dt", j), ("Dv", j)]
-    o += [("T", 0), ("Xs", 0), ("Xa", 0), ("Xb", 0), ("RgBC", 0), ("Q", 0), ("QB", 0), ("RgA2", 0), ("RgA1", 0), ("QA", 0)]
-    for j in range(NT):
-        o += [("Mb", j), ("Sg", j), ("Pt", j), ("Gt", j)]
-        if j in SPLIT_STORES:
-            o += [("ST", j)]
-        if j + 1 < NT:
-            o += [("T", j + 1), ("Xs", j + 1), ("Q", j + 1), ("Xa", j + 1), ("Xb", j + 1)]
-        o += [("Pv", j), ("Gv", j)]
-        if j in SPLIT_STORES:
-            o += [("SV", j)]
-        o += [("Ma", j), ("Re", j), ("C", j)]
-        o += [("SS", j)] if j in SPLIT_STORES else [("St", j)]
+        for w in STEP.split():
+            name = w.replace("+", "")
+            ahead = len(w) - len(name)
+            if name in ("Dt", "Dv") and j + ahead in STRIDED:
+                continue
+            put(name, j + ahead)
     return o
 
 
+STORE_AFTER = {"Gt": "ST", "Gv": "SV", "C": "SS"}
+HEAD = "T0 Xs0 Xa0 Xb0 RgBC0 QB0 Q0 RgA20 RgA10 Mb0 Sg0 QA0 Pt0 Pv0 Gt0 T1 Xs1 Gv0 Q1 Xa1 Xb1 Ma0 Re0 C0"
+STEP = "Mb Dt++ Sg T+ Xs+ Q+ Xa+ Pt Gt Pv Xb+ Ma Gv Re Dv++ C"
 ORDER = make_order()
 
 C0 = 1.0 / math.sqrt(512.0)
@@ -135,17 +137,14 @@ def tile_equivariantmlpblock_kernel(tc, x, W0, W1, W2, out):
         def deint_t(j):
             tdj = work.tile([P, 5, 128], BF16, name="td")
             src = xs[j][:, 1280:1920].rearrange("p (i m) -> p m i", m=5)
-            if j == 0:
-                nc.vector.tensor_copy(out=tdj[:], in_=src)
-            else:
-                nc.gpsimd.tensor_scalar(out=tdj[:], in0=src, scalar1=1.0, scalar2=0.0, op0=ALU.mult, op1=ALU.add)
+            nc.gpsimd.tensor_scalar(out=tdj[:], in0=src, scalar1=1.0, scalar2=0.0, op0=ALU.mult, op1=ALU.add)
             td[j] = tdj
 
         def deint_v(j):
             vdj = work.tile([P, 768], BF16, name="vd")
             dst = vdj[:].bitcast(F32).rearrange("p (r j) -> p r j", r=3)
             src = xs[j][:, 512:1280].bitcast(F32).rearrange("p (j r) -> p r j", r=3)
-            (nc.vector if j == 0 else nc.gpsimd).tensor_copy(out=dst, in_=src)
+            nc.vector.tensor_copy(out=dst, in_=src)
             vd[j] = vdj
 
         def t_src(j, m):

@@ -17,36 +17,38 @@ NT = 8
 D = 1920
 FLOPS = 2 * 1024 * (512 * 896 + 3 * 256 * 256 + 5 * 128 * 128)
 
-STRIDED_V = (0, 1)
-STRIDED = (0, 1)
+STRIDED_V = tuple(range(NT))
+STRIDED = (0,)
 GADD = ()
 A_SPLIT = 320
 def make_order():
-    o = [("L", 0), ("L", 100), ("L", 101), ("L", 102)] + [("L", j) for j in range(1, NT)] + [("ID", 0)]
+    o = [("L", 0), ("L", 100), ("L", 1), ("L", 101), ("L", 102)] + [("L", j) for j in range(2, NT)] + [("ID", 0)]
     done = set()
 
     def put(name, j):
-        if j < NT and (name, j) not in done:
+        if 0 <= j < NT and (name, j) not in done:
             done.add((name, j))
             o.append((name, j))
             if name in STORE_AFTER:
                 o.append((STORE_AFTER[name], j))
 
+    put("Dt", 1)
+    put("Dt", 2)
     for w in HEAD.split():
         put(w[:-1], int(w[-1]))
-    for j in range(NT):
+    for j in range(NT + 1):
         for w in STEP.split():
-            name = w.replace("+", "")
-            ahead = len(w) - len(name)
-            if name in ("Dt", "Dv") and j + ahead in STRIDED:
+            name = w.replace("+", "").replace("-", "")
+            ahead = (len(w) - len(name)) * (-1 if "-" in w else 1)
+            if name == "Dt" and j + ahead in STRIDED or name == "Dv" and j + ahead in STRIDED_V:
                 continue
             put(name, j + ahead)
     return o
 
 
 STORE_AFTER = {"Gt": "ST", "Gv": "SV", "C": "SS"}
-HEAD = "T0 Xs0 Xa0 Xb0 RgBC0 QB0 Q0 RgA20 RgA10 Mb0 Sg0 QA0 Pt0 Pv0 Gt0 T1 Xs1 Gv0 Q1 Xa1 Xb1 Ma0 Re0 C0"
-STEP = "Mb Dt++ Sg T+ Xs+ Q+ Xa+ Pt Gt Pv Xb+ Ma Gv Re Dv++ C"
+HEAD = "T0 Xs0 Xa0 Xb0 RgBC0 Q0 QB0 RgA10 RgA20 T1 QA0 Pt0"
+STEP = "Mb T+ Dt+++ Xs+ Sg Pt Q+ Xa+ Xb+ Pv Gt Gv Ma Re C"
 ORDER = make_order()
 
 C0 = 1.0 / math.sqrt(512.0)

@@ -16,44 +16,34 @@ P = 128
 NT = 8
 D = 1920
 FLOPS = 2 * 1024 * (512 * 896 + 3 * 256 * 256 + 5 * 128 * 128)
-
-STRIDED_V = tuple(range(NT))
-STRIDED = (0,)
-GADD = ()
+STRIDED_T = (0, 1)
+STRIDED_V = (0, 1, 2)
 A_SPLIT = 320
+LOADS = "x0 wb x1 wa w12 x2 x3 x4 x5 x6 x7"
+HEAD = "T0 Xs0 Xa0 Xb0 RgBC0 Q0 QB0 RgA10 RgA20 T1 QA0 Pt0"
+STEP = "Mb T+ Xs+ Sg Pt Q+ Ga+ Dt++ Dt+++ Dv+++ Xa+ Xb+ Pv Gt Gv Ma Re C"
+C0 = 1.0 / math.sqrt(512.0)
+C1 = 1.0 / 16.0
+C2 = 1.0 / math.sqrt(128.0)
+
+
 def make_order():
-    o = [("L", 0), ("L", 100), ("L", 1), ("L", 101), ("L", 102)] + [("L", j) for j in range(2, NT)] + [("ID", 0)]
-    done = set()
+    o = []
 
     def put(name, j):
-        if 0 <= j < NT and (name, j) not in done:
-            done.add((name, j))
-            o.append((name, j))
-            if name in STORE_AFTER:
-                o.append((STORE_AFTER[name], j))
+        if j < 0 or j >= NT or (name, j) in o:
+            return
+        if name == "Dt" and j in STRIDED_T or name == "Dv" and j in STRIDED_V:
+            return
+        o.append((name, j))
 
-    put("Dt", 1)
-    put("Dt", 2)
     for w in HEAD.split():
         put(w[:-1], int(w[-1]))
     for j in range(NT + 1):
         for w in STEP.split():
             name = w.replace("+", "").replace("-", "")
-            ahead = (len(w) - len(name)) * (-1 if "-" in w else 1)
-            if name == "Dt" and j + ahead in STRIDED or name == "Dv" and j + ahead in STRIDED_V:
-                continue
-            put(name, j + ahead)
+            put(name, j + (len(w) - len(name)) * (-1 if "-" in w else 1))
     return o
-
-
-STORE_AFTER = {"Gt": "ST", "Gv": "SV", "C": "SS"}
-HEAD = "T0 Xs0 Xa0 Xb0 RgBC0 Q0 QB0 RgA10 RgA20 T1 QA0 Pt0"
-STEP = "Mb T+ Dt+++ Xs+ Sg Pt Q+ Xa+ Xb+ Pv Gt Gv Ma Re C"
-ORDER = make_order()
-
-C0 = 1.0 / math.sqrt(512.0)
-C1 = 1.0 / 16.0
-C2 = 1.0 / math.sqrt(128.0)
 
 
 def tile_equivariantmlpblock_kernel(tc, x, W0, W1, W2, out):
@@ -77,32 +67,35 @@ def tile_equivariantmlpblock_kernel(tc, x, W0, W1, W2, out):
         w0v = W0.rearrange("(u p e) c -> u p e c", u=2, p=P, e=2)
 
         def load(what):
-            if what == 100:
+            if what == "wb":
                 for u in range(2):
                     nc.sync.dma_start(out=w0rb[:, 2 * u:2 * u + 2, :], in_=w0v[u, :, :, 512:896])
-            elif what == 101:
+            elif what == "wa":
                 for u in range(2):
                     nc.sync.dma_start(out=w0ra[:, 2 * u:2 * u + 2, :], in_=w0v[u, :, :, 0:512])
-            elif what == 102:
+            elif what == "w12":
                 nc.sync.dma_start(out=w1[:].rearrange("p e o -> p (e o)"), in_=W1.rearrange("(j e) o -> j (e o)", e=2))
                 nc.sync.dma_start(out=w2[:], in_=W2)
             else:
-                nc.sync.dma_start(out=xs[what][:], in_=xv[:, what, :])
+                j = int(what[1:])
+                nc.sync.dma_start(out=xs[j][:], in_=xv[:, j, :])
+
+        for what in LOADS.split():
+            load(what)
 
         idf = keep.tile([P, P], F32, name="idf")
         idb = keep.tile([P, P], BF16, name="idb")
         warm = keep.tile([P, 1], F32, name="warm")
         warm2 = keep.tile([P, 1], F32, name="warm2")
-
-        def consts(unused):
-            make_identity(nc, idf[:])
-            make_identity(nc, idb[:])
-            nc.vector.memset(warm[:], 0.0)
-            nc.scalar.activation(out=warm2[:], in_=warm[:], func=ACT.Sigmoid)
+        make_identity(nc, idf[:])
+        make_identity(nc, idb[:])
+        nc.vector.memset(warm[:], 0.0)
+        nc.scalar.activation(out=warm2[:], in_=warm[:], func=ACT.Sigmoid)
 
         w0g = keep.tile([P, 896, 4], BF16, name="w0g", align_bytes=64)
         w0c = keep.tile([P, 896], U32, name="w0c", align_bytes=64)
         w0s = keep.tile([P, 896], U8, name="w0s", align_bytes=64)
+        gate = keep.tile([P, NT], U32, name="gate")
 
         def regroup(copy_fn, raw, base, lo, hi):
             copy_fn(
@@ -112,10 +105,8 @@ def tile_equivariantmlpblock_kernel(tc, x, W0, W1, W2, out):
 
         def quant_w(lo, hi):
             nc.vector.quantize_mx(
-                out=w0c[:, lo:hi].bitcast(FP8X4),
-                scales=w0s[:, lo:hi],
-                in_=w0g[:, lo:hi, :].rearrange("p c t -> p (c t)"),
-            )
+                out=w0c[:, lo:hi].bitcast(FP8X4), scales=w0s[:, lo:hi],
+                in_=w0g[:, lo:hi, :].rearrange("p c t -> p (c t)"))
 
         def rg_bc(unused):
             regroup(nc.vector.tensor_copy, w0rb, 512, 512, 896)
@@ -135,30 +126,6 @@ def tile_equivariantmlpblock_kernel(tc, x, W0, W1, W2, out):
 
         vd = {}
         td = {}
-
-        def deint_t(j):
-            tdj = work.tile([P, 5, 128], BF16, name="td")
-            src = xs[j][:, 1280:1920].rearrange("p (i m) -> p m i", m=5)
-            nc.gpsimd.tensor_scalar(out=tdj[:], in0=src, scalar1=1.0, scalar2=0.0, op0=ALU.mult, op1=ALU.add)
-            td[j] = tdj
-
-        def deint_v(j):
-            vdj = work.tile([P, 768], BF16, name="vd")
-            dst = vdj[:].bitcast(F32).rearrange("p (r j) -> p r j", r=3)
-            src = xs[j][:, 512:1280].bitcast(F32).rearrange("p (j r) -> p r j", r=3)
-            nc.vector.tensor_copy(out=dst, in_=src)
-            vd[j] = vdj
-
-        def t_src(j, m):
-            if j in STRIDED:
-                return xs[j][:, 1280:1920].rearrange("p (i m) -> p m i", m=5)[:, m, :]
-            return td[j][:, m, :]
-
-        def v_src(j, r):
-            if j in STRIDED_V:
-                return xs[j][:, 512:1280].bitcast(F32).rearrange("p (j r) -> p r j", r=3)[:, r, :]
-            return vd[j][:].bitcast(F32)[:, 128 * r:128 * r + 128]
-
         tb = {}
         ua = {}
         ub = {}
@@ -172,25 +139,50 @@ def tile_equivariantmlpblock_kernel(tc, x, W0, W1, W2, out):
         pvb = {}
         ptb = {}
 
+        def st_Ga(j):
+            nc.gpsimd.tensor_copy(out=gate[:, j:j + 1], in_=sc[j][:, 0:1])
+
+        def deint_t(j):
+            tdj = work.tile([P, 5, 128], BF16, name="td")
+            nc.gpsimd.tensor_scalar(
+                out=tdj[:], in0=xs[j][:, 1280:1920].rearrange("p (i m) -> p m i", m=5),
+                scalar1=1.0, scalar2=0.0, op0=ALU.mult, op1=ALU.add)
+            td[j] = tdj
+
+        def deint_v(j):
+            vdj = work.tile([P, 3, 128], F32, name="vd")
+            nc.gpsimd.tensor_copy(
+                out=vdj[:], in_=xs[j][:, 512:1280].bitcast(F32).rearrange("p (j r) -> p r j", r=3))
+            vd[j] = vdj
+
+        def t_src(j, m):
+            if j in STRIDED_T:
+                return xs[j][:, 1280:1920].rearrange("p (i m) -> p m i", m=5)[:, m, :]
+            return td[j][:, m, :]
+
+        def v_src(j, r):
+            if j in STRIDED_V:
+                return xs[j][:, 512:1280].bitcast(F32).rearrange("p (j r) -> p r j", r=3)[:, r, :]
+            return vd[j][:, r, :]
+
         def st_T(j):
             t1 = psum.tile([P, 512], F32, name="t1")
             t2 = psum.tile([P, 512], F32, name="t2")
             xw = xs[j][:, 0:512].bitcast(F32)
             for u in range(2):
                 nc.tensor.transpose(t1[:, 128 * u:128 * u + 128], xw[:, 128 * u:128 * u + 128], idf[:])
-            for m in range(4):
-                nc.tensor.transpose(t1[:, 256 + 64 * m:320 + 64 * m].bitcast(BF16), t_src(j, m), idb[:])
-            nc.tensor.transpose(t2[:, 384:448].bitcast(BF16), t_src(j, 4), idb[:])
-            for r in range(3):
-                nc.tensor.transpose(t2[:, 128 * r:128 * r + 128], v_src(j, r), idf[:])
+            for r in range(2):
+                nc.tensor.transpose(t1[:, 256 + 128 * r:384 + 128 * r], v_src(j, r), idf[:])
+            nc.tensor.transpose(t2[:, 0:128], v_src(j, 2), idf[:])
+            for m in range(5):
+                nc.tensor.transpose(t2[:, 128 + 64 * m:192 + 64 * m].bitcast(BF16), t_src(j, m), idb[:])
             tb[j] = (t1, t2)
 
         def st_Xs(j):
             g = work.tile([P, 512], BF16, name="gs", align_bytes=64)
             nc.scalar.copy(
                 out=g[:].bitcast(F32).rearrange("p (n u) -> p n u", u=2),
-                in_=tb[j][0][:, 0:256].rearrange("p (u n) -> p n u", u=2),
-            )
+                in_=tb[j][0][:, 0:256].rearrange("p (u n) -> p n u", u=2))
             gs[j] = g
 
         def st_Xa(j):
@@ -245,19 +237,25 @@ def tile_equivariantmlpblock_kernel(tc, x, W0, W1, W2, out):
         def st_C(j):
             o = get_o(j)
             nc.vector.scalar_tensor_tensor(
-                out=o[:, 0:512], in0=pab[j][:], scalar=0.01 * C0, in1=o[:, 0:512],
-                op0=ALU.mult, op1=ALU.add)
+                out=o[:, 0:512], in0=pab[j][:], scalar=0.01 * C0, in1=o[:, 0:512], op0=ALU.mult, op1=ALU.add)
+            store(j, 0, 512)
+
+        def store(j, lo, hi):
+            nc.sync.dma_start(out=ov[:, j, lo:hi], in_=osb[j][:, lo:hi])
+
+        def v_lhsT(j, k):
+            r = k // 2
+            pairs = ua[j][:, 256 * r:256 * r + 256] if r < 2 else ub[j][:, 0:256]
+            return pairs.rearrange("p (n e) -> p e n", e=2)[:, k % 2, :]
 
         def st_Pv(j):
-            uv = ub[j][:, 0:768].rearrange("p (r n e) -> p r n e", r=3, e=2)
             banks = []
             for h in range(2):
                 pv = psum.tile([P, 512], F32, name="pv%d" % h)
                 for m in range(3):
                     for par in range(2):
-                        k = 3 * par + m
                         nc.tensor.matmul(
-                            out=pv[:, 128 * m:128 * m + 128], lhsT=uv[:, k // 2, :, k % 2],
+                            out=pv[:, 128 * m:128 * m + 128], lhsT=v_lhsT(j, 3 * par + m),
                             rhs=w1[:, par, 128 * h:128 * h + 128], start=(par == 0), stop=(par == 1))
                 banks.append(pv)
             pvb[j] = banks
@@ -267,9 +265,8 @@ def tile_equivariantmlpblock_kernel(tc, x, W0, W1, W2, out):
             for h in range(2):
                 pt = psum.tile([P, 512], F32, name="pt%d" % h)
                 for m in range(5):
-                    lhsT = ua[j][:, 128 * m:128 * m + 128] if m < 4 else ub[j][:, 768:896]
                     nc.tensor.matmul(
-                        out=pt[:, 64 * m:64 * m + 64], lhsT=lhsT,
+                        out=pt[:, 64 * m:64 * m + 64], lhsT=ub[j][:, 256 + 128 * m:384 + 128 * m],
                         rhs=w2[:, 64 * h:64 * h + 64], start=True, stop=True)
                 banks.append(pt)
             ptb[j] = banks
@@ -283,6 +280,10 @@ def tile_equivariantmlpblock_kernel(tc, x, W0, W1, W2, out):
                     scalar=C1,
                     in1=gates[j][:, 128 * h:128 * h + 128].unsqueeze(2).to_broadcast([P, 128, 3]),
                     op0=ALU.mult, op1=ALU.mult)
+                if j == NT - 1:
+                    store(j, 512 + 384 * h, 896 + 384 * h)
+            if j < NT - 1:
+                store(j, 512, 1280)
 
         def st_Gt(j):
             o = get_o(j)
@@ -293,24 +294,16 @@ def tile_equivariantmlpblock_kernel(tc, x, W0, W1, W2, out):
                     scalar=C2,
                     in1=gates[j][:, 256 + 64 * h:320 + 64 * h].unsqueeze(2).to_broadcast([P, 64, 5]),
                     op0=ALU.mult, op1=ALU.mult)
-
-        def st_St(j):
-            nc.sync.dma_start(out=ov[:, j, :], in_=osb[j][:])
-
-        def st_SS(j):
-            nc.sync.dma_start(out=ov[:, j, 0:512], in_=osb[j][:, 0:512])
-
-        def st_SV(j):
-            nc.sync.dma_start(out=ov[:, j, 512:1280], in_=osb[j][:, 512:1280])
-
-        def st_ST(j):
-            nc.sync.dma_start(out=ov[:, j, 1280:1920], in_=osb[j][:, 1280:1920])
+                if j == NT - 1:
+                    store(j, 1280 + 320 * h, 1600 + 320 * h)
+            if j < NT - 1:
+                store(j, 1280, 1920)
 
         funcs = {
-            "L": load, "ID": consts, "RgBC": rg_bc, "RgA1": rg_a1, "RgA2": rg_a2, "QB": q_b, "QA": q_a,
+            "RgBC": rg_bc, "RgA1": rg_a1, "RgA2": rg_a2, "QB": q_b, "QA": q_a, "Ga": st_Ga,
             "Dt": deint_t, "Dv": deint_v, "T": st_T, "Xs": st_Xs, "Xa": st_Xa, "Xb": st_Xb, "Q": st_Q,
             "Mb": st_Mb, "Sg": st_Sg, "Ma": st_Ma, "Re": st_Re, "C": st_C, "Pv": st_Pv, "Pt": st_Pt,
-            "Gv": st_Gv, "Gt": st_Gt, "St": st_St, "SS": st_SS, "SV": st_SV, "ST": st_ST,
+            "Gv": st_Gv, "Gt": st_Gt,
         }
-        for name, j in ORDER:
+        for name, j in make_order():
             funcs[name](j)

@@ -18,9 +18,9 @@ D = 1920
 FLOPS = 2 * 1024 * (512 * 896 + 3 * 256 * 256 + 5 * 128 * 128)
 STRIDED_T = (0, 1)
 STRIDED_V = (0, 1, 2)
-A_SPLIT = 320
+A_SPLIT = 352
 LOADS = "x0 wb x1 wa w12 x2 x3 x4 x5 x6 x7"
-HEAD = "T0 Xs0 Xa0 Xb0 RgBC0 Q0 QB0 RgA10 RgA20 T1 QA0 Pt0"
+HEAD = "T0 Xs0 Xa0 Xb0 RgBC0 Q0 QB0 RgA10 RgA20 T1 QA0 Mb0 Pt0"
 STEP = "Mb T+ Xs+ Sg Pt Q+ Ga+ Dt++ Dt+++ Dv+++ Xa+ Xb+ Pv Gt Gv Ma Re C"
 C0 = 1.0 / math.sqrt(512.0)
 C1 = 1.0 / 16.0
@@ -112,7 +112,8 @@ def tile_equivariantmlpblock_kernel(tc, x, W0, W1, W2, out):
             regroup(nc.vector.tensor_copy, w0rb, 512, 512, 896)
 
         def rg_a1(unused):
-            regroup(nc.vector.tensor_copy, w0ra, 0, 0, A_SPLIT)
+            regroup(nc.vector.tensor_copy, w0ra, 0, 0, 256)
+            regroup(nc.vector.tensor_copy, w0ra, 0, 256, A_SPLIT)
 
         def rg_a2(unused):
             regroup(nc.scalar.copy, w0ra, 0, A_SPLIT, 512)
@@ -122,7 +123,8 @@ def tile_equivariantmlpblock_kernel(tc, x, W0, W1, W2, out):
             quant_w(768, 896)
 
         def q_a(unused):
-            quant_w(0, 512)
+            quant_w(0, 256)
+            quant_w(256, 512)
 
         vd = {}
         td = {}
@@ -226,7 +228,7 @@ def tile_equivariantmlpblock_kernel(tc, x, W0, W1, W2, out):
             return osb[j]
 
         def st_Ma(j):
-            pa = psum.tile([P, 512], F32, name="pa")
+            pa = psum.tile([P, 512], F32, name="t1" if j == NT - 1 else "pa")
             mx(j, pa[:], 0, 512)
             pab[j] = pa
 

import math
from contextlib import ExitStack

import concourse.mybir as mybir
from concourse.masks import make_identity

BF16 = mybir.dt.bfloat16
F32 = mybir.dt.float32
U32 = mybir.dt.uint32
U8 = mybir.dt.uint8
FP8X4 = mybir.dt.float8_e4m3fn_x4
ACT = mybir.ActivationFunctionType
ALU = mybir.AluOpType

P = 128
NT = 8
D = 1920
FLOPS = 2 * 1024 * (512 * 896 + 3 * 256 * 256 + 5 * 128 * 128)
STRIDED_T = (0, 1)
STRIDED_V = (0, 1, 2)
A_SPLIT = 352
LOADS = "x0 wb x1 wa w12 x2 x3 x4 x5 x6 x7"
HEAD = "T0 Xs0 Xa0 Xb0 RgBC0 Q0 QB0 RgA10 RgA20 T1 QA0 Mb0 Pt0"
STEP = "Mb T+ Xs+ Sg Pt Q+ Ga+ Dt++ Dt+++ Dv+++ Xa+ Xb+ Pv Gt Gv Ma Re C"
C0 = 1.0 / math.sqrt(512.0)
C1 = 1.0 / 16.0
C2 = 1.0 / math.sqrt(128.0)


def make_order():
    o = []

    def put(name, j):
        if j < 0 or j >= NT or (name, j) in o:
            return
        if name == "Dt" and j in STRIDED_T or name == "Dv" and j in STRIDED_V:
            return
        o.append((name, j))

    for w in HEAD.split():
        put(w[:-1], int(w[-1]))
    for j in range(NT + 1):
        for w in STEP.split():
            name = w.replace("+", "").replace("-", "")
            put(name, j + (len(w) - len(name)) * (-1 if "-" in w else 1))
    return o


def tile_equivariantmlpblock_kernel(tc, x, W0, W1, W2, out):
    nc = tc.nc
    xv = x.rearrange("(p t) c -> p t c", t=NT)
    ov = out.rearrange("(p t) c -> p t c", t=NT)
    with ExitStack() as ctx:
        keep = ctx.enter_context(tc.tile_pool(name="keep", bufs=1))
        work = ctx.enter_context(tc.tile_pool(name="work", bufs=NT))
        psum = ctx.enter_context(tc.psum_pool(name="psum", bufs=1))
        ctx.enter_context(tc.manual_schedule())

        xs = []
        for j in range(NT):
            xj = keep.tile([P, D], BF16, name="x%d" % j, align_bytes=64)
            xs.append(xj)
        w0ra = keep.tile([P, 4, 512], BF16, name="w0ra", align_bytes=64)
        w0rb = keep.tile([P, 4, 384], BF16, name="w0rb", align_bytes=64)
        w1 = keep.tile([P, 2, 256], BF16, name="w1")
        w2 = keep.tile([P, 128], BF16, name="w2")
        w0v = W0.rearrange("(u p e) c -> u p e c", u=2, p=P, e=2)

        def load(what):
            if what == "wb":
                for u in range(2):
                    nc.sync.dma_start(out=w0rb[:, 2 * u:2 * u + 2, :], in_=w0v[u, :, :, 512:896])
            elif what == "wa":
                for u in range(2):
                    nc.sync.dma_start(out=w0ra[:, 2 * u:2 * u + 2, :], in_=w0v[u, :, :, 0:512])
            elif what == "w12":
                nc.sync.dma_start(out=w1[:].rearrange("p e o -> p (e o)"), in_=W1.rearrange("(j e) o -> j (e o)", e=2))
                nc.sync.dma_start(out=w2[:], in_=W2)
            else:
                j = int(what[1:])
                nc.sync.dma_start(out=xs[j][:], in_=xv[:, j, :])

        for what in LOADS.split():
            load(what)

        idf = keep.tile([P, P], F32, name="idf")
        idb = keep.tile([P, P], BF16, name="idb")
        warm = keep.tile([P, 1], F32, name="warm")
        warm2 = keep.tile([P, 1], F32, name="warm2")
        make_identity(nc, idf[:])
        make_identity(nc, idb[:])
        nc.vector.memset(warm[:], 0.0)
        nc.scalar.activation(out=warm2[:], in_=warm[:], func=ACT.Sigmoid)

        w0g = keep.tile([P, 896, 4], BF16, name="w0g", align_bytes=64)
        w0c = keep.tile([P, 896], U32, name="w0c", align_bytes=64)
        w0s = keep.tile([P, 896], U8, name="w0s", align_bytes=64)
        gate = keep.tile([P, NT], U32, name="gate")

        def regroup(copy_fn, raw, base, lo, hi):
            copy_fn(
                out=w0g[:, lo:hi, :].rearrange("p (c i) t -> p c t i", i=4),
                in_=raw[:, :, lo - base:hi - base].rearrange("p t (c i) -> p c t i", i=4),
            )

        def quant_w(lo, hi):
            nc.vector.quantize_mx(
                out=w0c[:, lo:hi].bitcast(FP8X4), scales=w0s[:, lo:hi],
                in_=w0g[:, lo:hi, :].rearrange("p c t -> p (c t)"))

        def rg_bc(unused):
            regroup(nc.vector.tensor_copy, w0rb, 512, 512, 896)

        def rg_a1(unused):
            regroup(nc.vector.tensor_copy, w0ra, 0, 0, 256)
            regroup(nc.vector.tensor_copy, w0ra, 0, 256, A_SPLIT)

        def rg_a2(unused):
            regroup(nc.scalar.copy, w0ra, 0, A_SPLIT, 512)

        def q_b(unused):
            quant_w(512, 768)
            quant_w(768, 896)

        def q_a(unused):
            quant_w(0, 256)
            quant_w(256, 512)

        vd = {}
        td = {}
        tb = {}
        ua = {}
        ub = {}
        gs = {}
        sc = {}
        ss = {}
        gates = {}
        osb = {}
        pab = {}
        pbb = {}
        pvb = {}
        ptb = {}

        def st_Ga(j):
            nc.gpsimd.tensor_copy(out=gate[:, j:j + 1], in_=sc[j][:, 0:1])

        def deint_t(j):
            tdj = work.tile([P, 5, 128], BF16, name="td")
            nc.gpsimd.tensor_scalar(
                out=tdj[:], in0=xs[j][:, 1280:1920].rearrange("p (i m) -> p m i", m=5),
                scalar1=1.0, scalar2=0.0, op0=ALU.mult, op1=ALU.add)
            td[j] = tdj

        def deint_v(j):
            vdj = work.tile([P, 3, 128], F32, name="vd")
            nc.gpsimd.tensor_copy(
                out=vdj[:], in_=xs[j][:, 512:1280].bitcast(F32).rearrange("p (j r) -> p r j", r=3))
            vd[j] = vdj

        def t_src(j, m):
            if j in STRIDED_T:
                return xs[j][:, 1280:1920].rearrange("p (i m) -> p m i", m=5)[:, m, :]
            return td[j][:, m, :]

        def v_src(j, r):
            if j in STRIDED_V:
                return xs[j][:, 512:1280].bitcast(F32).rearrange("p (j r) -> p r j", r=3)[:, r, :]
            return vd[j][:, r, :]

        def st_T(j):
            t1 = psum.tile([P, 512], F32, name="t1")
            t2 = psum.tile([P, 512], F32, name="t2")
            xw = xs[j][:, 0:512].bitcast(F32)
            for u in range(2):
                nc.tensor.transpose(t1[:, 128 * u:128 * u + 128], xw[:, 128 * u:128 * u + 128], idf[:])
            for r in range(2):
                nc.tensor.transpose(t1[:, 256 + 128 * r:384 + 128 * r], v_src(j, r), idf[:])
            nc.tensor.transpose(t2[:, 0:128], v_src(j, 2), idf[:])
            for m in range(5):
                nc.tensor.transpose(t2[:, 128 + 64 * m:192 + 64 * m].bitcast(BF16), t_src(j, m), idb[:])
            tb[j] = (t1, t2)

        def st_Xs(j):
            g = work.tile([P, 512], BF16, name="gs", align_bytes=64)
            nc.scalar.copy(
                out=g[:].bitcast(F32).rearrange("p (n u) -> p n u", u=2),
                in_=tb[j][0][:, 0:256].rearrange("p (u n) -> p n u", u=2))
            gs[j] = g

        def st_Xa(j):
            uaj = work.tile([P, 512], BF16, name="ua")
            nc.scalar.copy(out=uaj[:].bitcast(F32), in_=tb[j][0][:, 256:512])
            ua[j] = uaj

        def st_Xb(j):
            ubj = work.tile([P, 896], BF16, name="ub")
            nc.scalar.copy(out=ubj[:].bitcast(F32), in_=tb[j][1][:, 0:448])
            ub[j] = ubj

        def st_Q(j):
            scj = work.tile([P, 128], U32, name="sc", align_bytes=64)
            ssj = work.tile([P, 128], U8, name="ss", align_bytes=64)
            nc.vector.quantize_mx(out=scj[:].bitcast(FP8X4), scales=ssj[:], in_=gs[j][:])
            sc[j] = scj
            ss[j] = ssj

        def mx(j, acc, lo, hi):
            nc.tensor.matmul_mx(
                out=acc, lhsT=sc[j][:].bitcast(FP8X4), lhsT_scale=ss[j][:],
                rhs=w0c[:, lo:hi].bitcast(FP8X4), rhs_scale=w0s[:, lo:hi],
                start=True, stop=True)

        def st_Mb(j):
            pb = psum.tile([P, 512], F32, name="pb")
            mx(j, pb[:, 0:256], 512, 768)
            mx(j, pb[:, 256:384], 768, 896)
            pbb[j] = pb

        def st_Sg(j):
            g = work.tile([P, 384], F32, name="g")
            nc.scalar.activation(out=g[:], in_=pbb[j][:, 0:384], func=ACT.Sigmoid, scale=C0)
            gates[j] = g

        def get_o(j):
            if j not in osb:
                o = work.tile([P, D], F32, name="o")
                osb[j] = o
            return osb[j]

        def st_Ma(j):
            pa = psum.tile([P, 512], F32, name="t1" if j == NT - 1 else "pa")
            mx(j, pa[:], 0, 512)
            pab[j] = pa

        def st_Re(j):
            o = get_o(j)
            nc.scalar.activation(out=o[:, 0:512], in_=pab[j][:], func=ACT.Relu, scale=0.99 * C0)

        def st_C(j):
            o = get_o(j)
            nc.vector.scalar_tensor_tensor(
                out=o[:, 0:512], in0=pab[j][:], scalar=0.01 * C0, in1=o[:, 0:512], op0=ALU.mult, op1=ALU.add)
            store(j, 0, 512)

        def store(j, lo, hi):
            nc.sync.dma_start(out=ov[:, j, lo:hi], in_=osb[j][:, lo:hi])

        def v_lhsT(j, k):
            r = k // 2
            pairs = ua[j][:, 256 * r:256 * r + 256] if r < 2 else ub[j][:, 0:256]
            return pairs.rearrange("p (n e) -> p e n", e=2)[:, k % 2, :]

        def st_Pv(j):
            banks = []
            for h in range(2):
                pv = psum.tile([P, 512], F32, name="pv%d" % h)
                for m in range(3):
                    for par in range(2):
                        nc.tensor.matmul(
                            out=pv[:, 128 * m:128 * m + 128], lhsT=v_lhsT(j, 3 * par + m),
                            rhs=w1[:, par, 128 * h:128 * h + 128], start=(par == 0), stop=(par == 1))
                banks.append(pv)
            pvb[j] = banks

        def st_Pt(j):
            banks = []
            for h in range(2):
                pt = psum.tile([P, 512], F32, name="pt%d" % h)
                for m in range(5):
                    nc.tensor.matmul(
                        out=pt[:, 64 * m:64 * m + 64], lhsT=ub[j][:, 256 + 128 * m:384 + 128 * m],
                        rhs=w2[:, 64 * h:64 * h + 64], start=True, stop=True)
                banks.append(pt)
            ptb[j] = banks

        def st_Gv(j):
            o = get_o(j)
            for h in range(2):
                nc.vector.scalar_tensor_tensor(
                    out=o[:, 512 + 384 * h:896 + 384 * h].rearrange("p (o m) -> p o m", m=3),
                    in0=pvb[j][h][:, 0:384].rearrange("p (m o) -> p o m", m=3),
                    scalar=C1,
                    in1=gates[j][:, 128 * h:128 * h + 128].unsqueeze(2).to_broadcast([P, 128, 3]),
                    op0=ALU.mult, op1=ALU.mult)
                if j == NT - 1:
                    store(j, 512 + 384 * h, 896 + 384 * h)
            if j < NT - 1:
                store(j, 512, 1280)

        def st_Gt(j):
            o = get_o(j)
            for h in range(2):
                nc.vector.scalar_tensor_tensor(
                    out=o[:, 1280 + 320 * h:1600 + 320 * h].rearrange("p (o m) -> p o m", m=5),
                    in0=ptb[j][h][:, 0:320].rearrange("p (m o) -> p o m", m=5),
                    scalar=C2,
                    in1=gates[j][:, 256 + 64 * h:320 + 64 * h].unsqueeze(2).to_broadcast([P, 64, 5]),
                    op0=ALU.mult, op1=ALU.mult)
                if j == NT - 1:
                    store(j, 1280 + 320 * h, 1600 + 320 * h)
            if j < NT - 1:
                store(j, 1280, 1920)

        funcs = {
            "RgBC": rg_bc, "RgA1": rg_a1, "RgA2": rg_a2, "QB": q_b, "QA": q_a, "Ga": st_Ga,
            "Dt": deint_t, "Dv": deint_v, "T": st_T, "Xs": st_Xs, "Xa": st_Xa, "Xb": st_Xb, "Q": st_Q,
            "Mb": st_Mb, "Sg": st_Sg, "Ma": st_Ma, "Re": st_Re, "C": st_C, "Pv": st_Pv, "Pt": st_Pt,
            "Gv": st_Gv, "Gt": st_Gt,
        }
        for name, j in make_order():
            funcs[name](j)
